import numpy as np
import ml_dtypes


def mxq(x, axis, fmt="e4m3"):
    dtype, down = {"e4m3": (ml_dtypes.float8_e4m3fn, 7), "e5m2": (ml_dtypes.float8_e5m2, 14)}[fmt]
    v = np.moveaxis(np.asarray(x, np.float32).astype(ml_dtypes.bfloat16).astype(np.float64), axis, -1)
    blocks = v.reshape(v.shape[:-1] + (-1, 32))
    amax = np.abs(blocks).max(-1, keepdims=True)
    byte = np.maximum(np.where(amax > 0, np.frexp(amax)[1] - 1 + 127, 0) - down, 1)
    scale = np.exp2(byte - 127.0)
    codes = (blocks / scale).astype(np.float32).astype(dtype).astype(np.float64)
    return np.moveaxis((codes * scale).reshape(v.shape), -1, axis)


WIDE = False


def mx_kscale(k):
    if not WIDE:
        return np.ones(k)
    levels = np.array([10, -10, 5, -5, 0])
    a = np.random.permutation(np.resize(levels, k // 512 * 4)).reshape(k // 512, 4)
    idx = np.arange(k)
    return np.exp2(a[idx // 512, idx % 128 // 32])


BF16 = ml_dtypes.bfloat16


def bf(x):
    return np.asarray(x, np.float32).astype(BF16)


def f64(x):
    return np.asarray(x).astype(np.float64)


NB, T, N, H, HD, CO = 2, 4, 512, 4, 128, 1024
B = NB * T
C = H * HD
VS = 10.0 * H / N


def setup_inputs():
    t = mx_kscale(C)
    sg = np.sign(np.random.standard_normal(C))
    return {"q": bf(np.random.standard_normal((B, H, N, HD)) * 1.5),
            "k": bf(np.random.standard_normal((B, H, N, HD)) * 1.5),
            "v": bf(np.abs(np.random.standard_normal((B, H, N, HD))) * VS * (sg * t).reshape(H, HD)[None, :, None, :]),
            "w_proj": bf(np.random.standard_normal((CO, C)) * 0.5 / np.sqrt(C) / t[None, :])}


def reference(q, k, v, w_proj):
    s = f64(q) @ f64(k).transpose(0, 1, 3, 2) * HD ** -0.5
    e = np.exp(s - s.max(1, keepdims=True))
    attn = e / e.sum(1, keepdims=True)
    o = mxq(attn, 3, "e4m3") @ mxq(f64(v), 2, "e4m3")
    o = o.transpose(0, 2, 1, 3).reshape(B, N, C)
    wq = mxq(f64(w_proj), 1, "e4m3")
    return mxq(o, 2, "e4m3") @ wq.T

@@ -1,0 +1,241 @@
+from contextlib import ExitStack
+
+import concourse.mybir as mybir
+from concourse.masks import make_identity
+
+BF16 = mybir.dt.bfloat16
+F32 = mybir.dt.float32
+U32 = mybir.dt.uint32
+U8 = mybir.dt.uint8
+FP8X4 = mybir.dt.float8_e4m3fn_x4
+ACT = mybir.ActivationFunctionType
+ALU = mybir.AluOpType
+AXIS = mybir.AxisListType
+
+P = 128
+PACK = 4
+FRAMES, HEADS, TOKENS, HEAD_DIM, OUT_CH = 8, 4, 512, 128, 1024
+CHANNELS = HEADS * HEAD_DIM
+TILES = TOKENS // P
+BANK = 512
+SCALE = HEAD_DIM**-0.5
+CHUNKS = FRAMES * TILES
+
+LAG_SUM = 1
+LAG_NORMALISE = 6
+LAG_ATTEND = 7
+LAG_REGROUP = 8
+LAG_PROJECT = 9
+LAG_STORE = 10
+
+FLOPS = 2 * FRAMES * HEADS * TOKENS * TOKENS * HEAD_DIM * 2 + 2 * FRAMES * TOKENS * CHANNELS * OUT_CH
+
+
+def quantise(nc, codes, scales, grouped):
+    nc.vector.quantize_mx(out=codes.bitcast(FP8X4), scales=scales, in_=grouped)
+
+
+def mx_pass(nc, acc, lhs_codes, lhs_scales, rhs_codes, rhs_scales):
+    nc.tensor.matmul_mx(
+        out=acc,
+        lhsT=lhs_codes.bitcast(FP8X4),
+        lhsT_scale=lhs_scales,
+        rhs=rhs_codes.bitcast(FP8X4),
+        rhs_scale=rhs_scales,
+        start=True,
+        stop=True,
+    )
+
+
+def tile_attention2_pa_t_kernel(tc, q, k, v, w_proj, out):
+    nc = tc.nc
+    with ExitStack() as stack:
+        stack.enter_context(tc.manual_schedule())
+        const = stack.enter_context(tc.tile_pool(name="const", bufs=1))
+        pair_pool = stack.enter_context(tc.tile_pool(name="pair_pool", bufs=2))
+        ring = stack.enter_context(tc.tile_pool(name="ring", bufs=3))
+        deep = stack.enter_context(tc.tile_pool(name="deep", bufs=LAG_NORMALISE + 2))
+        psum_s = stack.enter_context(tc.psum_pool(name="psum_s", bufs=TILES))
+        psum_tr = stack.enter_context(tc.psum_pool(name="psum_tr", bufs=1))
+        psum_o = stack.enter_context(tc.psum_pool(name="psum_o", bufs=1))
+        psum_out = stack.enter_context(tc.psum_pool(name="psum_out", bufs=OUT_CH // BANK))
+
+        ident = const.tile([P, P], BF16)
+        make_identity(nc, ident[:])
+        w_rows = const.tile([P, OUT_CH // P, CHANNELS], BF16)
+        w_grouped = const.tile([P, OUT_CH, PACK], BF16, align_bytes=64)
+        w_codes = const.tile([P, OUT_CH], U32, align_bytes=64)
+        w_scales = const.tile([P, OUT_CH], U8, align_bytes=64)
+
+        rows_of, turned_of, v_mx_of, total_of, inverse_of = {}, {}, {}, {}, {}
+        s_of, e_of, attn_of, o_ps_of, o_grouped_of, out_ps_of = {}, {}, {}, {}, {}, {}
+
+        def load_frame(b):
+            k_rows = pair_pool.tile([P, HEADS, TILES, HEAD_DIM], BF16)
+            q_rows = pair_pool.tile([P, HEADS, TILES, HEAD_DIM], BF16)
+            v_rows = pair_pool.tile([P, HEADS, PACK, HEAD_DIM], BF16)
+            for rows, src in ((k_rows, k), (q_rows, q), (v_rows, v)):
+                nc.sync.dma_start(
+                    out=rows[:].rearrange("p h j d -> p h (j d)"),
+                    in_=src[b].rearrange("h (p j) d -> p h (j d)", j=TILES),
+                )
+            rows_of[b] = (k_rows, q_rows, v_rows)
+
+        def turn_quarter(b, quarter):
+            if quarter == 0:
+                kT = pair_pool.tile([P, HEADS, TILES, P], BF16)
+                qT = pair_pool.tile([P, HEADS, TILES, P], BF16)
+                turned_of[b] = (kT, qT)
+            rows, turned = rows_of[b][quarter // 2], turned_of[b][quarter // 2]
+            first = 2 * (quarter % 2)
+            tr_ps = psum_tr.tile([P, 2, TILES, P], BF16, tag="tr")
+            for i in range(2):
+                for j in range(TILES):
+                    nc.tensor.transpose(out=tr_ps[:, i, j, :], in_=rows[:, first + i, j, :], identity=ident[:])
+            nc.scalar.copy(out=turned[:, first : first + 2, :, :], in_=tr_ps[:])
+
+        def quantise_v(b):
+            v_rows = rows_of[b][2]
+            v_grouped = const.tile([P, HEADS, HEAD_DIM, PACK], BF16, align_bytes=64)
+            nc.gpsimd.tensor_scalar(
+                out=v_grouped[:], in0=v_rows[:].rearrange("p h t d -> p h d t"),
+                scalar1=1.0, scalar2=0.0, op0=ALU.mult, op1=ALU.add,
+            )
+            v_codes = ring.tile([P, HEADS * HEAD_DIM], U32, align_bytes=64)
+            v_scales = ring.tile([P, HEADS * HEAD_DIM], U8, align_bytes=64)
+            quantise(nc, v_codes[:], v_scales[:], v_grouped[:].rearrange("p h d t -> p (h d t)"))
+            v_mx_of[b] = (v_codes, v_scales)
+
+        def turn_w(g):
+            w_ps = psum_tr.tile([P, PACK, P], BF16, tag="tr")
+            for t in range(PACK):
+                nc.tensor.transpose(out=w_ps[:, t, :], in_=w_rows[:, g, t * P : (t + 1) * P], identity=ident[:])
+            nc.scalar.copy(out=w_grouped[:, g * P : (g + 1) * P, :], in_=w_ps[:].rearrange("p t c -> p c t"))
+
+        def score_matmuls(c):
+            kT, qT = turned_of[c // TILES]
+            s_of[c] = []
+            for t in range(TILES):
+                s_ps = psum_s.tile([P, HEADS, P], F32)
+                for h in range(HEADS):
+                    nc.tensor.matmul(out=s_ps[:, h, :], lhsT=kT[:, h, t, :], rhs=qT[:, h, c % TILES, :], start=True, stop=True)
+                s_of[c].append(s_ps)
+
+        def exponentials(c):
+            tops = []
+            for t in range(TILES):
+                top = deep.tile([P, P], F32)
+                nc.vector.tensor_reduce(out=top[:], in_=s_of[c][t][:].rearrange("p h n -> p n h"), axis=AXIS.X, op=ALU.max)
+                tops.append(top)
+            e = deep.tile([P, TILES, HEADS, P], F32)
+            for t in range(TILES):
+                nc.vector.tensor_tensor(
+                    out=e[:, t, :, :], in0=s_of[c][t][:],
+                    in1=tops[t][:].unsqueeze(1).to_broadcast([P, HEADS, P]), op=ALU.subtract,
+                )
+            e_flat = e[:].rearrange("p t h n -> p (t h n)")
+            nc.scalar.activation(out=e_flat, in_=e_flat, func=ACT.Exp, scale=SCALE)
+            e_of[c] = e
+
+        def add_head_pairs(c):
+            pair_sum = pair_pool.tile([P, TILES, 2, P], F32)
+            nc.vector.tensor_tensor(out=pair_sum[:], in0=e_of[c][:, :, 0:2, :], in1=e_of[c][:, :, 2:4, :], op=ALU.add)
+            return pair_sum
+
+        def add_pair_sums(c, pair_sum):
+            if c % TILES == 0:
+                total = pair_pool.tile([P, TILES, TILES, P], F32)
+                total_of[c // TILES] = total
+            nc.vector.tensor_tensor(
+                out=total_of[c // TILES][:, c % TILES, :, :], in0=pair_sum[:, :, 0, :], in1=pair_sum[:, :, 1, :], op=ALU.add
+            )
+
+        def invert_totals(b):
+            total = total_of[b][:].rearrange("p j t n -> p (j t n)")
+            nc.scalar.activation(out=total, in_=total, func=ACT.Ln)
+            inverse = pair_pool.tile([P, TILES, TILES, P], F32)
+            nc.scalar.activation(out=inverse[:].rearrange("p j t n -> p (j t n)"), in_=total, func=ACT.Exp, scale=-1.0)
+            inverse_of[b] = inverse
+
+        def normalise(c):
+            attn = ring.tile([P, HEADS, P, PACK], BF16, align_bytes=64)
+            for h in range(HEADS):
+                nc.gpsimd.tensor_tensor(
+                    out=attn[:, h, :, :], in0=e_of[c][:, :, h, :].rearrange("p t n -> p n t"),
+                    in1=inverse_of[c // TILES][:, c % TILES, :, :].rearrange("p t n -> p n t"), op=ALU.mult,
+                )
+            attn_of[c] = attn
+
+        def attend(c):
+            attn_codes = pair_pool.tile([P, HEADS * P], U32, align_bytes=64)
+            attn_scales = pair_pool.tile([P, HEADS * P], U8, align_bytes=64)
+            quantise(nc, attn_codes[:], attn_scales[:], attn_of[c][:].rearrange("p h n t -> p (h n t)"))
+            v_codes, v_scales = v_mx_of[c // TILES]
+            o_ps = psum_o.tile([P, HEADS, P], F32)
+            for h in range(HEADS):
+                cols = slice(h * P, (h + 1) * P)
+                mx_pass(nc, o_ps[:, h, :], v_codes[:, cols], v_scales[:, cols], attn_codes[:, cols], attn_scales[:, cols])
+            o_ps_of[c] = o_ps
+
+        def regroup_o(c):
+            o_grouped = ring.tile([P, P, PACK], BF16, align_bytes=64)
+            nc.scalar.copy(out=o_grouped[:], in_=o_ps_of[c][:].rearrange("p h n -> p n h"))
+            o_grouped_of[c] = o_grouped
+
+        def project(c):
+            o_codes = pair_pool.tile([P, P], U32, align_bytes=64)
+            o_scales = pair_pool.tile([P, P], U8, align_bytes=64)
+            quantise(nc, o_codes[:], o_scales[:], o_grouped_of[c][:].rearrange("p n h -> p (n h)"))
+            out_ps_of[c] = []
+            for half in range(OUT_CH // BANK):
+                cols = slice(half * BANK, (half + 1) * BANK)
+                out_ps = psum_out.tile([P, BANK], F32)
+                mx_pass(nc, out_ps[:], o_codes[:], o_scales[:], w_codes[:, cols], w_scales[:, cols])
+                out_ps_of[c].append(out_ps)
+
+        def store(c):
+            out_rows = ring.tile([P, OUT_CH], F32)
+            for half in range(OUT_CH // BANK):
+                nc.scalar.copy(out=out_rows[:, half * BANK : (half + 1) * BANK], in_=out_ps_of[c][half][:])
+            nc.sync.dma_start(out=out[c // TILES].rearrange("(p j) c -> p j c", j=TILES)[:, c % TILES, :], in_=out_rows[:])
+
+        load_frame(0)
+        nc.sync.dma_start(out=w_rows[:], in_=w_proj.rearrange("(g p) c -> p g c", p=P))
+        load_frame(1)
+        for quarter in range(4):
+            turn_quarter(0, quarter)
+        score_matmuls(0)
+
+        for step in range(CHUNKS + LAG_STORE):
+            b, j = step // TILES, step % TILES
+            if 0 <= step - LAG_REGROUP < CHUNKS:
+                regroup_o(step - LAG_REGROUP)
+            if 0 <= step - LAG_STORE < CHUNKS:
+                store(step - LAG_STORE)
+            if b + 1 < FRAMES:
+                turn_quarter(b + 1, j)
+            if step < OUT_CH // P:
+                turn_w(step)
+            if step < CHUNKS:
+                exponentials(step)
+            if step + 1 < CHUNKS:
+                score_matmuls(step + 1)
+            if j == 0 and b < FRAMES:
+                quantise_v(b)
+            if j == 0 and b + 2 < FRAMES:
+                load_frame(b + 2)
+            if step == OUT_CH // P:
+                quantise(nc, w_codes[:], w_scales[:], w_grouped[:].rearrange("p c t -> p (c t)"))
+            summed = 0 <= step - LAG_SUM < CHUNKS
+            if summed:
+                pair_sum = add_head_pairs(step - LAG_SUM)
+            if 0 <= step - LAG_ATTEND < CHUNKS:
+                attend(step - LAG_ATTEND)
+            if summed:
+                add_pair_sums(step - LAG_SUM, pair_sum)
+            if 0 <= step - LAG_PROJECT < CHUNKS:
+                project(step - LAG_PROJECT)
+            if summed and (step - LAG_SUM) % TILES == TILES - 1:
+                invert_totals((step - LAG_SUM) // TILES)
+            if 0 <= step - LAG_NORMALISE < CHUNKS:
+                normalise(step - LAG_NORMALISE)

@@ -160,7 +160,7 @@ def tile_attention2_pa_t_kernel(tc, q, k, v, w_proj, out):
         def normalise(c):
             attn = ring.tile([P, HEADS, P, PACK], BF16, align_bytes=64)
             for h in range(HEADS):
-                nc.gpsimd.tensor_tensor(
+                nc.vector.tensor_tensor(
                     out=attn[:, h, :, :], in0=e_of[c][:, :, h, :].rearrange("p t n -> p n t"),
                     in1=inverse_of[c // TILES][:, c % TILES, :, :].rearrange("p t n -> p n t"), op=ALU.mult,
                 )

@@ -127,43 +127,42 @@ def tile_attention2_pa_t_kernel(tc, q, k, v, w_proj, out):
                 top = deep.tile([P, P], F32)
                 nc.vector.tensor_reduce(out=top[:], in_=s_of[c][t][:].rearrange("p h n -> p n h"), axis=AXIS.X, op=ALU.max)
                 tops.append(top)
-            e = deep.tile([P, TILES, HEADS, P], F32)
+            shifted = pair_pool.tile([P, PACK, HEADS, P], F32)
             for t in range(TILES):
                 nc.vector.tensor_tensor(
-                    out=e[:, t, :, :], in0=s_of[c][t][:],
+                    out=shifted[:, t, :, :], in0=s_of[c][t][:],
                     in1=tops[t][:].unsqueeze(1).to_broadcast([P, HEADS, P]), op=ALU.subtract,
                 )
-            e_flat = e[:].rearrange("p t h n -> p (t h n)")
-            nc.scalar.activation(out=e_flat, in_=e_flat, func=ACT.Exp, scale=SCALE)
+            e = deep.tile([P, HEADS, P, PACK], F32)
+            nc.scalar.activation(out=e[:], in_=shifted[:].rearrange("p t h n -> p h n t"), func=ACT.Exp, scale=SCALE)
             e_of[c] = e
 
         def add_head_pairs(c):
-            pair_sum = pair_pool.tile([P, TILES, 2, P], F32)
-            nc.vector.tensor_tensor(out=pair_sum[:], in0=e_of[c][:, :, 0:2, :], in1=e_of[c][:, :, 2:4, :], op=ALU.add)
+            pair_sum = pair_pool.tile([P, 2, P, PACK], F32)
+            nc.vector.tensor_tensor(out=pair_sum[:], in0=e_of[c][:, 0:2, :, :], in1=e_of[c][:, 2:4, :, :], op=ALU.add)
             return pair_sum
 
         def add_pair_sums(c, pair_sum):
             if c % TILES == 0:
-                total = pair_pool.tile([P, TILES, TILES, P], F32)
+                total = pair_pool.tile([P, TILES, P, PACK], F32)
                 total_of[c // TILES] = total
             nc.vector.tensor_tensor(
-                out=total_of[c // TILES][:, c % TILES, :, :], in0=pair_sum[:, :, 0, :], in1=pair_sum[:, :, 1, :], op=ALU.add
+                out=total_of[c // TILES][:, c % TILES, :, :], in0=pair_sum[:, 0, :, :], in1=pair_sum[:, 1, :, :], op=ALU.add
             )
 
         def invert_totals(b):
-            total = total_of[b][:].rearrange("p j t n -> p (j t n)")
+            total = total_of[b][:].rearrange("p j n t -> p (j n t)")
             nc.scalar.activation(out=total, in_=total, func=ACT.Ln)
-            inverse = pair_pool.tile([P, TILES, TILES, P], F32)
-            nc.scalar.activation(out=inverse[:].rearrange("p j t n -> p (j t n)"), in_=total, func=ACT.Exp, scale=-1.0)
+            inverse = pair_pool.tile([P, TILES, P, PACK], F32)
+            nc.scalar.activation(out=inverse[:].rearrange("p j n t -> p (j n t)"), in_=total, func=ACT.Exp, scale=-1.0)
             inverse_of[b] = inverse
 
         def normalise(c):
             attn = ring.tile([P, HEADS, P, PACK], BF16, align_bytes=64)
-            for h in range(HEADS):
-                nc.vector.tensor_tensor(
-                    out=attn[:, h, :, :], in0=e_of[c][:, :, h, :].rearrange("p t n -> p n t"),
-                    in1=inverse_of[c // TILES][:, c % TILES, :, :].rearrange("p t n -> p n t"), op=ALU.mult,
-                )
+            nc.vector.tensor_tensor(
+                out=attn[:], in0=e_of[c][:],
+                in1=inverse_of[c // TILES][:, c % TILES, :, :].unsqueeze(1).to_broadcast([P, HEADS, P, PACK]), op=ALU.mult,
+            )
             attn_of[c] = attn
 
         def attend(c):

@@ -137,16 +137,14 @@ def tile_attention2_pa_t_kernel(tc, q, k, v, w_proj, out):
             nc.scalar.activation(out=e[:], in_=shifted[:].rearrange("p t h n -> p h n t"), func=ACT.Exp, scale=SCALE)
             e_of[c] = e
 
-        def add_head_pairs(c):
-            pair_sum = pair_pool.tile([P, 2, P, PACK], F32)
-            nc.vector.tensor_tensor(out=pair_sum[:], in0=e_of[c][:, 0:2, :, :], in1=e_of[c][:, 2:4, :, :], op=ALU.add)
-            return pair_sum
-
-        def add_pair_sums(c, pair_sum):
+        def add_heads(c):
             if c % TILES == 0:
                 total = pair_pool.tile([P, TILES, P, PACK], F32)
                 total_of[c // TILES] = total
-            nc.vector.tensor_tensor(
+            pair_sum = pair_pool.tile([P, 2, P, PACK], F32)
+            for i in range(2):
+                nc.gpsimd.tensor_tensor(out=pair_sum[:, i, :, :], in0=e_of[c][:, i, :, :], in1=e_of[c][:, i + 2, :, :], op=ALU.add)
+            nc.gpsimd.tensor_tensor(
                 out=total_of[c // TILES][:, c % TILES, :, :], in0=pair_sum[:, 0, :, :], in1=pair_sum[:, 1, :, :], op=ALU.add
             )
 
@@ -225,16 +223,13 @@ def tile_attention2_pa_t_kernel(tc, q, k, v, w_proj, out):
                 load_frame(b + 2)
             if step == OUT_CH // P:
                 quantise(nc, w_codes[:], w_scales[:], w_grouped[:].rearrange("p c t -> p (c t)"))
-            summed = 0 <= step - LAG_SUM < CHUNKS
-            if summed:
-                pair_sum = add_head_pairs(step - LAG_SUM)
+            if 0 <= step - LAG_SUM < CHUNKS:
+                add_heads(step - LAG_SUM)
+                if (step - LAG_SUM) % TILES == TILES - 1:
+                    invert_totals((step - LAG_SUM) // TILES)
             if 0 <= step - LAG_ATTEND < CHUNKS:
                 attend(step - LAG_ATTEND)
-            if summed:
-                add_pair_sums(step - LAG_SUM, pair_sum)
             if 0 <= step - LAG_PROJECT < CHUNKS:
                 project(step - LAG_PROJECT)
-            if summed and (step - LAG_SUM) % TILES == TILES - 1:
-                invert_totals((step - LAG_SUM) // TILES)
             if 0 <= step - LAG_NORMALISE < CHUNKS:
                 normalise(step - LAG_NORMALISE)

@@ -127,14 +127,14 @@ def tile_attention2_pa_t_kernel(tc, q, k, v, w_proj, out):
                 top = deep.tile([P, P], F32)
                 nc.vector.tensor_reduce(out=top[:], in_=s_of[c][t][:].rearrange("p h n -> p n h"), axis=AXIS.X, op=ALU.max)
                 tops.append(top)
-            shifted = pair_pool.tile([P, PACK, HEADS, P], F32)
+            below = pair_pool.tile([P, PACK, HEADS, P], F32)
             for t in range(TILES):
                 nc.vector.tensor_tensor(
-                    out=shifted[:, t, :, :], in0=s_of[c][t][:],
-                    in1=tops[t][:].unsqueeze(1).to_broadcast([P, HEADS, P]), op=ALU.subtract,
+                    out=below[:, t, :, :], in0=tops[t][:].unsqueeze(1).to_broadcast([P, HEADS, P]),
+                    in1=s_of[c][t][:], op=ALU.subtract,
                 )
             e = deep.tile([P, HEADS, P, PACK], F32)
-            nc.scalar.activation(out=e[:], in_=shifted[:].rearrange("p t h n -> p h n t"), func=ACT.Exp, scale=SCALE)
+            nc.scalar.activation(out=e[:], in_=below[:].rearrange("p t h n -> p h n t"), func=ACT.Exp, scale=-SCALE)
             e_of[c] = e
 
         def add_heads(c):

@@ -22,6 +22,7 @@ SCALE = HEAD_DIM**-0.5
 CHUNKS = FRAMES * TILES
 
 LAG_SUM = 1
+LAG_INVERT = 5
 LAG_NORMALISE = 6
 LAG_ATTEND = 7
 LAG_REGROUP = 8
@@ -67,7 +68,7 @@ def tile_attention2_pa_t_kernel(tc, q, k, v, w_proj, out):
         w_codes = const.tile([P, OUT_CH], U32, align_bytes=64)
         w_scales = const.tile([P, OUT_CH], U8, align_bytes=64)
 
-        rows_of, turned_of, v_mx_of, total_of, inverse_of = {}, {}, {}, {}, {}
+        rows_of, turned_of, v_mx_of, total_of, log_total_of, inverse_of = {}, {}, {}, {}, {}, {}
         s_of, e_of, attn_of, o_ps_of, o_grouped_of, out_ps_of = {}, {}, {}, {}, {}, {}
 
         def load_frame(b):
@@ -81,14 +82,14 @@ def tile_attention2_pa_t_kernel(tc, q, k, v, w_proj, out):
                 )
             rows_of[b] = (k_rows, q_rows, v_rows)
 
-        def turn_quarter(b, quarter):
+        def turn_quarter(b, quarter, banks):
             if quarter == 0:
                 kT = pair_pool.tile([P, HEADS, TILES, P], BF16)
                 qT = pair_pool.tile([P, HEADS, TILES, P], BF16)
                 turned_of[b] = (kT, qT)
             rows, turned = rows_of[b][quarter // 2], turned_of[b][quarter // 2]
             first = 2 * (quarter % 2)
-            tr_ps = psum_tr.tile([P, 2, TILES, P], BF16, tag="tr")
+            tr_ps = banks.tile([P, 2, TILES, P], BF16, tag="bank")
             for i in range(2):
                 for j in range(TILES):
                     nc.tensor.transpose(out=tr_ps[:, i, j, :], in_=rows[:, first + i, j, :], identity=ident[:])
@@ -107,7 +108,7 @@ def tile_attention2_pa_t_kernel(tc, q, k, v, w_proj, out):
             v_mx_of[b] = (v_codes, v_scales)
 
         def turn_w(g):
-            w_ps = psum_tr.tile([P, PACK, P], BF16, tag="tr")
+            w_ps = psum_tr.tile([P, PACK, P], BF16, tag="bank")
             for t in range(PACK):
                 nc.tensor.transpose(out=w_ps[:, t, :], in_=w_rows[:, g, t * P : (t + 1) * P], identity=ident[:])
             nc.scalar.copy(out=w_grouped[:, g * P : (g + 1) * P, :], in_=w_ps[:].rearrange("p t c -> p c t"))
@@ -116,7 +117,7 @@ def tile_attention2_pa_t_kernel(tc, q, k, v, w_proj, out):
             kT, qT = turned_of[c // TILES]
             s_of[c] = []
             for t in range(TILES):
-                s_ps = psum_s.tile([P, HEADS, P], F32)
+                s_ps = psum_s.tile([P, HEADS, P], F32, tag="bank")
                 for h in range(HEADS):
                     nc.tensor.matmul(out=s_ps[:, h, :], lhsT=kT[:, h, t, :], rhs=qT[:, h, c % TILES, :], start=True, stop=True)
                 s_of[c].append(s_ps)
@@ -127,14 +128,14 @@ def tile_attention2_pa_t_kernel(tc, q, k, v, w_proj, out):
                 top = deep.tile([P, P], F32)
                 nc.vector.tensor_reduce(out=top[:], in_=s_of[c][t][:].rearrange("p h n -> p n h"), axis=AXIS.X, op=ALU.max)
                 tops.append(top)
-            below = pair_pool.tile([P, PACK, HEADS, P], F32)
+            shifted = pair_pool.tile([P, PACK, HEADS, P], F32)
             for t in range(TILES):
                 nc.vector.tensor_tensor(
-                    out=below[:, t, :, :], in0=tops[t][:].unsqueeze(1).to_broadcast([P, HEADS, P]),
-                    in1=s_of[c][t][:], op=ALU.subtract,
+                    out=shifted[:, t, :, :], in0=s_of[c][t][:],
+                    in1=tops[t][:].unsqueeze(1).to_broadcast([P, HEADS, P]), op=ALU.subtract,
                 )
             e = deep.tile([P, HEADS, P, PACK], F32)
-            nc.scalar.activation(out=e[:], in_=below[:].rearrange("p t h n -> p h n t"), func=ACT.Exp, scale=-SCALE)
+            nc.scalar.activation(out=e[:], in_=shifted[:].rearrange("p t h n -> p h n t"), func=ACT.Exp, scale=SCALE)
             e_of[c] = e
 
         def add_heads(c):
@@ -148,18 +149,21 @@ def tile_attention2_pa_t_kernel(tc, q, k, v, w_proj, out):
                 out=total_of[c // TILES][:, c % TILES, :, :], in0=pair_sum[:, 0, :, :], in1=pair_sum[:, 1, :, :], op=ALU.add
             )
 
-        def invert_totals(b):
-            total = total_of[b][:].rearrange("p j n t -> p (j n t)")
-            nc.scalar.activation(out=total, in_=total, func=ACT.Ln)
-            inverse = pair_pool.tile([P, TILES, P, PACK], F32)
-            nc.scalar.activation(out=inverse[:].rearrange("p j n t -> p (j n t)"), in_=total, func=ACT.Exp, scale=-1.0)
-            inverse_of[b] = inverse
+        def log_totals(b):
+            log_total = const.tile([P, TILES, P, PACK], F32)
+            nc.scalar.activation(out=log_total[:], in_=total_of[b][:], func=ACT.Ln)
+            log_total_of[b] = log_total
+
+        def invert(c):
+            inverse = ring.tile([P, P, PACK], F32)
+            nc.scalar.activation(out=inverse[:], in_=log_total_of[c // TILES][:, c % TILES, :, :], func=ACT.Exp, scale=-1.0)
+            inverse_of[c] = inverse
 
         def normalise(c):
             attn = ring.tile([P, HEADS, P, PACK], BF16, align_bytes=64)
             nc.vector.tensor_tensor(
                 out=attn[:], in0=e_of[c][:],
-                in1=inverse_of[c // TILES][:, c % TILES, :, :].unsqueeze(1).to_broadcast([P, HEADS, P, PACK]), op=ALU.mult,
+                in1=inverse_of[c][:].unsqueeze(1).to_broadcast([P, HEADS, P, PACK]), op=ALU.mult,
             )
             attn_of[c] = attn
 
@@ -200,7 +204,7 @@ def tile_attention2_pa_t_kernel(tc, q, k, v, w_proj, out):
         nc.sync.dma_start(out=w_rows[:], in_=w_proj.rearrange("(g p) c -> p g c", p=P))
         load_frame(1)
         for quarter in range(4):
-            turn_quarter(0, quarter)
+            turn_quarter(0, quarter, psum_s)
         score_matmuls(0)
 
         for step in range(CHUNKS + LAG_STORE):
@@ -210,9 +214,11 @@ def tile_attention2_pa_t_kernel(tc, q, k, v, w_proj, out):
             if 0 <= step - LAG_STORE < CHUNKS:
                 store(step - LAG_STORE)
             if b + 1 < FRAMES:
-                turn_quarter(b + 1, j)
+                turn_quarter(b + 1, j, psum_tr)
             if step < OUT_CH // P:
                 turn_w(step)
+            if 0 <= step - LAG_INVERT < CHUNKS:
+                invert(step - LAG_INVERT)
             if step < CHUNKS:
                 exponentials(step)
             if step + 1 < CHUNKS:
@@ -226,7 +232,7 @@ def tile_attention2_pa_t_kernel(tc, q, k, v, w_proj, out):
             if 0 <= step - LAG_SUM < CHUNKS:
                 add_heads(step - LAG_SUM)
                 if (step - LAG_SUM) % TILES == TILES - 1:
-                    invert_totals((step - LAG_SUM) // TILES)
+                    log_totals((step - LAG_SUM) // TILES)
             if 0 <= step - LAG_ATTEND < CHUNKS:
                 attend(step - LAG_ATTEND)
             if 0 <= step - LAG_PROJECT < CHUNKS:

@@ -10,7 +10,6 @@ U8 = mybir.dt.uint8
 FP8X4 = mybir.dt.float8_e4m3fn_x4
 ACT = mybir.ActivationFunctionType
 ALU = mybir.AluOpType
-AXIS = mybir.AxisListType
 
 P = 128
 PACK = 4
@@ -20,14 +19,15 @@ TILES = TOKENS // P
 BANK = 512
 SCALE = HEAD_DIM**-0.5
 CHUNKS = FRAMES * TILES
+W_GROUPS = OUT_CH // P
 
-LAG_SUM = 1
-LAG_INVERT = 5
-LAG_NORMALISE = 6
-LAG_ATTEND = 7
-LAG_REGROUP = 8
-LAG_PROJECT = 9
-LAG_STORE = 10
+BATCH = TILES
+
+LAG_LOG = 3
+LAG_INVERT = LAG_LOG + BATCH
+LAG_NORMALISE = LAG_INVERT + 1
+LAG_ATTEND = LAG_NORMALISE + 1
+LAG_PROJECT = LAG_ATTEND + 1
 
 FLOPS = 2 * FRAMES * HEADS * TOKENS * TOKENS * HEAD_DIM * 2 + 2 * FRAMES * TOKENS * CHANNELS * OUT_CH
 
@@ -53,189 +53,293 @@ def tile_attention2_pa_t_kernel(tc, q, k, v, w_proj, out):
     with ExitStack() as stack:
         stack.enter_context(tc.manual_schedule())
         const = stack.enter_context(tc.tile_pool(name="const", bufs=1))
-        pair_pool = stack.enter_context(tc.tile_pool(name="pair_pool", bufs=2))
-        ring = stack.enter_context(tc.tile_pool(name="ring", bufs=3))
-        deep = stack.enter_context(tc.tile_pool(name="deep", bufs=LAG_NORMALISE + 2))
-        psum_s = stack.enter_context(tc.psum_pool(name="psum_s", bufs=TILES))
-        psum_tr = stack.enter_context(tc.psum_pool(name="psum_tr", bufs=1))
-        psum_o = stack.enter_context(tc.psum_pool(name="psum_o", bufs=1))
-        psum_out = stack.enter_context(tc.psum_pool(name="psum_out", bufs=OUT_CH // BANK))
+        two = stack.enter_context(tc.tile_pool(name="two", bufs=2))
+        three = stack.enter_context(tc.tile_pool(name="three", bufs=3))
+        deep = stack.enter_context(tc.tile_pool(name="deep", bufs=LAG_NORMALISE + 1))
+        psum = stack.enter_context(tc.psum_pool(name="psum", bufs=1))
 
         ident = const.tile([P, P], BF16)
         make_identity(nc, ident[:])
-        w_rows = const.tile([P, OUT_CH // P, CHANNELS], BF16)
-        w_grouped = const.tile([P, OUT_CH, PACK], BF16, align_bytes=64)
+        ident_f32 = const.tile([P, P], F32)
+        make_identity(nc, ident_f32[:])
         w_codes = const.tile([P, OUT_CH], U32, align_bytes=64)
         w_scales = const.tile([P, OUT_CH], U8, align_bytes=64)
+        w_rows = deep.tile([P, W_GROUPS, CHANNELS], BF16, align_bytes=64, tag="e")
+        w_grouped = deep.tile([P, OUT_CH, PACK], BF16, align_bytes=64, tag="e")
 
-        rows_of, turned_of, v_mx_of, total_of, log_total_of, inverse_of = {}, {}, {}, {}, {}, {}
-        s_of, e_of, attn_of, o_ps_of, o_grouped_of, out_ps_of = {}, {}, {}, {}, {}, {}
+        rows_of, turned_of, tr_ps_of, v_rows_of, v_grouped_of, v_mx_of = {}, {}, {}, {}, {}, {}
+        s_of, first_of, top_of, shifted_of, e_of, sums_of, inverse_of = {}, {}, {}, {}, {}, {}, {}
+        inv_ps_of, attn_of, o_ps_of, o_mx_of, out_ps_of, out_rows_of = {}, {}, {}, {}, {}, {}
 
-        def load_frame(b):
-            k_rows = pair_pool.tile([P, HEADS, TILES, HEAD_DIM], BF16)
-            q_rows = pair_pool.tile([P, HEADS, TILES, HEAD_DIM], BF16)
-            v_rows = pair_pool.tile([P, HEADS, PACK, HEAD_DIM], BF16)
-            for rows, src in ((k_rows, k), (q_rows, q), (v_rows, v)):
-                nc.sync.dma_start(
-                    out=rows[:].rearrange("p h j d -> p h (j d)"),
-                    in_=src[b].rearrange("h (p j) d -> p h (j d)", j=TILES),
-                )
-            rows_of[b] = (k_rows, q_rows, v_rows)
+        def ok(c):
+            return 0 <= c < CHUNKS
 
-        def turn_quarter(b, quarter, banks):
+        def load(rows, src, b, heads):
+            nc.sync.dma_start(
+                out=rows[:, heads].rearrange("p h j d -> p h (j d)"),
+                in_=src[b, heads].rearrange("h (p j) d -> p h (j d)", j=TILES),
+            )
+
+        def load_qk(b):
+            k_rows = two.tile([P, HEADS, TILES, HEAD_DIM], BF16)
+            q_rows = two.tile([P, HEADS, TILES, HEAD_DIM], BF16)
+            rows_of[b] = (k_rows, q_rows)
+            for i in range(2):
+                for rows, source in ((k_rows, k), (q_rows, q)):
+                    load(rows, source, b, slice(2 * i, 2 * i + 2))
+
+        def load_v(b):
+            v_rows = two.tile([P, HEADS, PACK, HEAD_DIM], BF16)
+            v_rows_of[b] = v_rows
+            load(v_rows, v, b, slice(0, HEADS))
+
+        def turn(b, quarter, bank):
             if quarter == 0:
-                kT = pair_pool.tile([P, HEADS, TILES, P], BF16)
-                qT = pair_pool.tile([P, HEADS, TILES, P], BF16)
+                kT = two.tile([P, HEADS, TILES, P], BF16)
+                qT = two.tile([P, HEADS, TILES, P], BF16)
                 turned_of[b] = (kT, qT)
-            rows, turned = rows_of[b][quarter // 2], turned_of[b][quarter // 2]
-            first = 2 * (quarter % 2)
-            tr_ps = banks.tile([P, 2, TILES, P], BF16, tag="bank")
+            rows, turned = rows_of[b][quarter % 2], turned_of[b][quarter % 2]
+            first = 2 * (quarter // 2)
+            tr_ps = psum.tile([P, 2, TILES, P], BF16, tag=bank)
             for i in range(2):
                 for j in range(TILES):
                     nc.tensor.transpose(out=tr_ps[:, i, j, :], in_=rows[:, first + i, j, :], identity=ident[:])
-            nc.scalar.copy(out=turned[:, first : first + 2, :, :], in_=tr_ps[:])
+            tr_ps_of[b, quarter] = (turned[:, first : first + 2, :, :], tr_ps)
 
-        def quantise_v(b):
-            v_rows = rows_of[b][2]
-            v_grouped = const.tile([P, HEADS, HEAD_DIM, PACK], BF16, align_bytes=64)
-            nc.gpsimd.tensor_scalar(
-                out=v_grouped[:], in0=v_rows[:].rearrange("p h t d -> p h d t"),
-                scalar1=1.0, scalar2=0.0, op0=ALU.mult, op1=ALU.add,
-            )
-            v_codes = ring.tile([P, HEADS * HEAD_DIM], U32, align_bytes=64)
-            v_scales = ring.tile([P, HEADS * HEAD_DIM], U8, align_bytes=64)
-            quantise(nc, v_codes[:], v_scales[:], v_grouped[:].rearrange("p h d t -> p (h d t)"))
-            v_mx_of[b] = (v_codes, v_scales)
+        def turned_copy(b, quarter):
+            turned, tr_ps = tr_ps_of[b, quarter]
+            nc.scalar.copy(out=turned, in_=tr_ps[:])
 
         def turn_w(g):
-            w_ps = psum_tr.tile([P, PACK, P], BF16, tag="bank")
+            w_ps = psum.tile([P, PACK, P], BF16, tag="o")
             for t in range(PACK):
                 nc.tensor.transpose(out=w_ps[:, t, :], in_=w_rows[:, g, t * P : (t + 1) * P], identity=ident[:])
             nc.scalar.copy(out=w_grouped[:, g * P : (g + 1) * P, :], in_=w_ps[:].rearrange("p t c -> p c t"))
 
-        def score_matmuls(c):
+        def group_v(b, h):
+            if h == 0:
+                v_grouped = two.tile([P, HEADS, HEAD_DIM, PACK], BF16, align_bytes=64)
+                v_grouped_of[b] = v_grouped
+            nc.vector.tensor_copy(out=v_grouped_of[b][:, h], in_=v_rows_of[b][:, h].rearrange("p t d -> p d t"))
+
+        def quantise_v(b, h):
+            if h == 0:
+                v_codes = three.tile([P, HEADS * HEAD_DIM], U32, align_bytes=64)
+                v_scales = three.tile([P, HEADS * HEAD_DIM], U8, align_bytes=64)
+                v_mx_of[b] = (v_codes, v_scales)
+            v_codes, v_scales = v_mx_of[b]
+            cols = slice(h * HEAD_DIM, (h + 1) * HEAD_DIM)
+            quantise(nc, v_codes[:, cols], v_scales[:, cols], v_grouped_of[b][:, h].rearrange("p d t -> p (d t)"))
+
+        def scores(c, h):
             kT, qT = turned_of[c // TILES]
-            s_of[c] = []
-            for t in range(TILES):
-                s_ps = psum_s.tile([P, HEADS, P], F32, tag="bank")
-                for h in range(HEADS):
-                    nc.tensor.matmul(out=s_ps[:, h, :], lhsT=kT[:, h, t, :], rhs=qT[:, h, c % TILES, :], start=True, stop=True)
-                s_of[c].append(s_ps)
+            s_ps = psum.tile([P, PACK, P], F32, tag=f"s{h}")
+            for t in range(PACK):
+                nc.tensor.matmul(out=s_ps[:, t, :], lhsT=kT[:, h, t, :], rhs=qT[:, h, c % TILES, :], start=True, stop=True)
+            s_of[c, h] = s_ps[:].rearrange("p t n -> p n t")
 
-        def exponentials(c):
-            tops = []
-            for t in range(TILES):
-                top = deep.tile([P, P], F32)
-                nc.vector.tensor_reduce(out=top[:], in_=s_of[c][t][:].rearrange("p h n -> p n h"), axis=AXIS.X, op=ALU.max)
-                tops.append(top)
-            shifted = pair_pool.tile([P, PACK, HEADS, P], F32)
-            for t in range(TILES):
-                nc.vector.tensor_tensor(
-                    out=shifted[:, t, :, :], in0=s_of[c][t][:],
-                    in1=tops[t][:].unsqueeze(1).to_broadcast([P, HEADS, P]), op=ALU.subtract,
-                )
-            e = deep.tile([P, HEADS, P, PACK], F32)
-            nc.scalar.activation(out=e[:], in_=shifted[:].rearrange("p t h n -> p h n t"), func=ACT.Exp, scale=SCALE)
-            e_of[c] = e
+        def copy_first(c):
+            first = two.tile([P, P, PACK], F32)
+            nc.vector.tensor_copy(out=first[:], in_=s_of[c, 0])
+            first_of[c] = first
 
-        def add_heads(c):
-            if c % TILES == 0:
-                total = pair_pool.tile([P, TILES, P, PACK], F32)
-                total_of[c // TILES] = total
-            pair_sum = pair_pool.tile([P, 2, P, PACK], F32)
-            for i in range(2):
-                nc.gpsimd.tensor_tensor(out=pair_sum[:, i, :, :], in0=e_of[c][:, i, :, :], in1=e_of[c][:, i + 2, :, :], op=ALU.add)
+        def maximum(c, h):
+            top = (two if h == HEADS - 1 else const).tile([P, P, PACK], F32, tag=f"top{h}")
+            before = first_of[c] if h == 1 else top_of[c]
+            nc.vector.tensor_tensor(out=top[:], in0=s_of[c, h], in1=before[:], op=ALU.max)
+            top_of[c] = top
+
+        def subtract(c, h):
+            shifted = three.tile([P, P, PACK], F32, tag=f"shifted{h}")
+            if h == 0:
+                nc.gpsimd.tensor_tensor(out=shifted[:], in0=first_of[c][:], in1=top_of[c][:], op=ALU.subtract)
+            else:
+                nc.vector.tensor_tensor(out=shifted[:], in0=s_of[c, h], in1=top_of[c][:], op=ALU.subtract)
+            shifted_of[c, h] = shifted
+
+        def exponential(c, h):
+            if c not in e_of:
+                e = deep.tile([P, HEADS, P, PACK], F32, align_bytes=64, tag="e")
+                e_of[c] = e
+            nc.scalar.activation(out=e_of[c][:, h], in_=shifted_of[c, h][:], func=ACT.Exp, scale=SCALE)
+
+        def add_pair(c, i, a, b):
+            if i == 0:
+                pair = const.tile([P, 2, P, PACK], F32)
+                sums_of[c] = pair
+            nc.gpsimd.tensor_tensor(out=sums_of[c][:, i], in0=e_of[c][:, a], in1=e_of[c][:, b], op=ALU.add)
+
+        def add_pairs(c):
+            total = deep.tile([P, P * PACK], F32)
+            pair = sums_of[c]
             nc.gpsimd.tensor_tensor(
-                out=total_of[c // TILES][:, c % TILES, :, :], in0=pair_sum[:, 0, :, :], in1=pair_sum[:, 1, :, :], op=ALU.add
+                out=total[:], in0=pair[:, 0].rearrange("p n t -> p (n t)"), in1=pair[:, 1].rearrange("p n t -> p (n t)"), op=ALU.add
             )
+            sums_of[c] = total
 
-        def log_totals(b):
-            log_total = const.tile([P, TILES, P, PACK], F32)
-            nc.scalar.activation(out=log_total[:], in_=total_of[b][:], func=ACT.Ln)
-            log_total_of[b] = log_total
+        def logarithm(c):
+            nc.scalar.activation(out=sums_of[c][:], in_=sums_of[c][:], func=ACT.Ln)
+
+        def turn_log(c):
+            log_ps = psum.tile([P, PACK, P], F32, tag="o")
+            for i in range(PACK):
+                nc.tensor.transpose(out=log_ps[:, i, :], in_=sums_of[c][:, i * P : (i + 1) * P], identity=ident_f32[:])
+            inverse = two.tile([P, PACK, P], F32)
+            inverse_of[c] = (log_ps, inverse)
 
         def invert(c):
-            inverse = ring.tile([P, P, PACK], F32)
-            nc.scalar.activation(out=inverse[:], in_=log_total_of[c // TILES][:, c % TILES, :, :], func=ACT.Exp, scale=-1.0)
-            inverse_of[c] = inverse
+            log_ps, inverse = inverse_of[c]
+            nc.scalar.activation(out=inverse[:], in_=log_ps[:], func=ACT.Exp, scale=-1.0)
 
-        def normalise(c):
-            attn = ring.tile([P, HEADS, P, PACK], BF16, align_bytes=64)
+        def turn_inverse(c):
+            inv_ps = psum.tile([P, PACK, P], F32, tag="inv")
+            for i in range(PACK):
+                nc.tensor.transpose(out=inv_ps[:, i, :], in_=inverse_of[c][1][:, i, :], identity=ident_f32[:])
+            inv_ps_of[c] = inv_ps
+
+        def normalise(c, h):
+            if h == 0:
+                attn = three.tile([P, HEADS, P * PACK], BF16, align_bytes=64)
+                attn_of[c] = attn
             nc.vector.tensor_tensor(
-                out=attn[:], in0=e_of[c][:],
-                in1=inverse_of[c][:].unsqueeze(1).to_broadcast([P, HEADS, P, PACK]), op=ALU.mult,
+                out=attn_of[c][:, h], in0=e_of[c][:, h].rearrange("p n t -> p (n t)"),
+                in1=inv_ps_of[c][:].rearrange("p i n -> p (i n)"), op=ALU.mult,
             )
-            attn_of[c] = attn
 
         def attend(c):
-            attn_codes = pair_pool.tile([P, HEADS * P], U32, align_bytes=64)
-            attn_scales = pair_pool.tile([P, HEADS * P], U8, align_bytes=64)
-            quantise(nc, attn_codes[:], attn_scales[:], attn_of[c][:].rearrange("p h n t -> p (h n t)"))
+            attn_codes = two.tile([P, HEADS * P], U32, align_bytes=64)
+            attn_scales = two.tile([P, HEADS * P], U8, align_bytes=64)
+            quantise(nc, attn_codes[:], attn_scales[:], attn_of[c][:].rearrange("p h m -> p (h m)"))
             v_codes, v_scales = v_mx_of[c // TILES]
-            o_ps = psum_o.tile([P, HEADS, P], F32)
+            o_ps = psum.tile([P, HEADS, P], F32, tag="o")
             for h in range(HEADS):
                 cols = slice(h * P, (h + 1) * P)
                 mx_pass(nc, o_ps[:, h, :], v_codes[:, cols], v_scales[:, cols], attn_codes[:, cols], attn_scales[:, cols])
             o_ps_of[c] = o_ps
 
         def regroup_o(c):
-            o_grouped = ring.tile([P, P, PACK], BF16, align_bytes=64)
+            o_grouped = three.tile([P, P, PACK], BF16, align_bytes=64)
             nc.scalar.copy(out=o_grouped[:], in_=o_ps_of[c][:].rearrange("p h n -> p n h"))
-            o_grouped_of[c] = o_grouped
+            o_ps_of[c] = o_grouped
 
-        def project(c):
-            o_codes = pair_pool.tile([P, P], U32, align_bytes=64)
-            o_scales = pair_pool.tile([P, P], U8, align_bytes=64)
-            quantise(nc, o_codes[:], o_scales[:], o_grouped_of[c][:].rearrange("p n h -> p (n h)"))
-            out_ps_of[c] = []
-            for half in range(OUT_CH // BANK):
-                cols = slice(half * BANK, (half + 1) * BANK)
-                out_ps = psum_out.tile([P, BANK], F32)
-                mx_pass(nc, out_ps[:], o_codes[:], o_scales[:], w_codes[:, cols], w_scales[:, cols])
-                out_ps_of[c].append(out_ps)
+        def quantise_o(c):
+            o_codes = two.tile([P, P], U32, align_bytes=64)
+            o_scales = two.tile([P, P], U8, align_bytes=64)
+            quantise(nc, o_codes[:], o_scales[:], o_ps_of[c][:].rearrange("p n h -> p (n h)"))
+            o_mx_of[c] = (o_codes, o_scales)
+
+        def project(c, half):
+            o_codes, o_scales = o_mx_of[c]
+            cols = slice(half * BANK, (half + 1) * BANK)
+            out_ps = psum.tile([P, BANK], F32, tag=f"out{half}")
+            mx_pass(nc, out_ps[:], o_codes[:], o_scales[:], w_codes[:, cols], w_scales[:, cols])
+            out_ps_of[c, half] = out_ps
+
+        def copy_out(c, half):
+            if half == 0:
+                out_rows = three.tile([P, OUT_CH], F32)
+                out_rows_of[c] = out_rows
+            nc.scalar.copy(out=out_rows_of[c][:, half * BANK : (half + 1) * BANK], in_=out_ps_of[c, half][:])
 
         def store(c):
-            out_rows = ring.tile([P, OUT_CH], F32)
-            for half in range(OUT_CH // BANK):
-                nc.scalar.copy(out=out_rows[:, half * BANK : (half + 1) * BANK], in_=out_ps_of[c][half][:])
-            nc.sync.dma_start(out=out[c // TILES].rearrange("(p j) c -> p j c", j=TILES)[:, c % TILES, :], in_=out_rows[:])
+            nc.sync.dma_start(out=out[c // TILES].rearrange("(p j) c -> p j c", j=TILES)[:, c % TILES, :], in_=out_rows_of[c][:])
 
-        load_frame(0)
+        turns = [(b, quarter) for b in range(1, FRAMES) for quarter in range(4)]
+
+        load_qk(0)
+        load_v(0)
         nc.sync.dma_start(out=w_rows[:], in_=w_proj.rearrange("(g p) c -> p g c", p=P))
-        load_frame(1)
+        load_qk(1)
         for quarter in range(4):
-            turn_quarter(0, quarter, psum_s)
-        score_matmuls(0)
+            turn(0, quarter, f"s{quarter}")
+            turned_copy(0, quarter)
+        for h in range(HEADS):
+            scores(0, h)
 
-        for step in range(CHUNKS + LAG_STORE):
+        exps = [(c, h) for c in range(CHUNKS) for h in (1, 2, 3, 0)]
+        adds = [(c, i) for c in range(CHUNKS) for i in range(3)]
+        done = added = 0
+        for step in range(CHUNKS + LAG_PROJECT + 1):
             b, j = step // TILES, step % TILES
-            if 0 <= step - LAG_REGROUP < CHUNKS:
-                regroup_o(step - LAG_REGROUP)
-            if 0 <= step - LAG_STORE < CHUNKS:
-                store(step - LAG_STORE)
-            if b + 1 < FRAMES:
-                turn_quarter(b + 1, j, psum_tr)
-            if step < OUT_CH // P:
-                turn_w(step)
-            if 0 <= step - LAG_INVERT < CHUNKS:
-                invert(step - LAG_INVERT)
-            if step < CHUNKS:
-                exponentials(step)
-            if step + 1 < CHUNKS:
-                score_matmuls(step + 1)
-            if j == 0 and b < FRAMES:
-                quantise_v(b)
+            c_inv, c_norm, c_att, c_proj = step - LAG_INVERT, step - LAG_NORMALISE, step - LAG_ATTEND, step - LAG_PROJECT
+            last = step - LAG_LOG
+            logs = list(range(last - BATCH + 1, last + 1)) if ok(last) and last % BATCH == BATCH - 1 else []
+            quota = (0, 5, 5, 6)[(step - LAG_LOG + 1) % BATCH] if step >= LAG_LOG - 1 else 4
+            todo = [x for x in exps[done : done + quota] if x[0] < step]
+            done_before = done
+            done += len(todo)
+            groups = (todo[:2], todo[2:])
+
+            def exp_group(i):
+                for c, h in groups[i]:
+                    exponential(c, h)
+
             if j == 0 and b + 2 < FRAMES:
-                load_frame(b + 2)
-            if step == OUT_CH // P:
+                load_qk(b + 2)
+            if j == 0 and b + 1 < FRAMES:
+                load_v(b + 1)
+            if ok(step):
+                copy_first(step)
+            if step < len(turns):
+                turn(*turns[step], "s0")
+            if step < len(turns):
+                turned_copy(*turns[step])
+            if ok(c_att):
+                normalise(c_att, 2)
+            if ok(step):
+                maximum(step, 1)
+            if ok(c_att):
+                normalise(c_att, 3)
+            if ok(c_norm):
+                turn_inverse(c_norm)
+            if ok(step):
+                maximum(step, 2)
+            if ok(c_att):
+                attend(c_att)
+            if ok(c_proj):
+                quantise_o(c_proj)
+                project(c_proj, 0)
+                project(c_proj, 1)
+            if ok(step - 1):
+                quantise_v((step - 1) // TILES, (step - 1) % TILES)
+            if b < FRAMES:
+                group_v(b, j)
+            if step < W_GROUPS // 2:
+                turn_w(2 * step)
+                turn_w(2 * step + 1)
+            if step == W_GROUPS // 2:
                 quantise(nc, w_codes[:], w_scales[:], w_grouped[:].rearrange("p c t -> p (c t)"))
-            if 0 <= step - LAG_SUM < CHUNKS:
-                add_heads(step - LAG_SUM)
-                if (step - LAG_SUM) % TILES == TILES - 1:
-                    log_totals((step - LAG_SUM) // TILES)
-            if 0 <= step - LAG_ATTEND < CHUNKS:
-                attend(step - LAG_ATTEND)
-            if 0 <= step - LAG_PROJECT < CHUNKS:
-                project(step - LAG_PROJECT)
-            if 0 <= step - LAG_NORMALISE < CHUNKS:
-                normalise(step - LAG_NORMALISE)
+            if ok(step):
+                maximum(step, 3)
+                subtract(step, 0)
+            for c, i in adds[added : added + 3]:
+                if exps.index((c, 2 if i == 0 else 0)) < done_before:
+                    if i < 2:
+                        add_pair(c, i, (1, 3)[i], (2, 0)[i])
+                    else:
+                        add_pairs(c)
+                    added += 1
+            if ok(c_norm):
+                normalise(c_norm, 0)
+            if ok(c_att):
+                regroup_o(c_att)
+            if ok(c_proj):
+                copy_out(c_proj, 0)
+                copy_out(c_proj, 1)
+                store(c_proj)
+            if ok(c_inv):
+                turn_log(c_inv)
+                invert(c_inv)
+            exp_group(0)
+            exp_group(1)
+            for c in logs:
+                logarithm(c)
+            if step + 1 < CHUNKS:
+                scores(step + 1, 0)
+            for h in range(1, HEADS):
+                if ok(step):
+                    subtract(step, h)
+                if step + 1 < CHUNKS:
+                    scores(step + 1, h)
+            if ok(c_norm):
+                normalise(c_norm, 1)

@@ -23,9 +23,9 @@ W_GROUPS = OUT_CH // P
 
 BATCH = TILES
 
-LAG_LOG = 3
-LAG_INVERT = LAG_LOG + BATCH
-LAG_NORMALISE = LAG_INVERT + 1
+LAG_LOG = 4
+LAG_TURN_LOG = LAG_LOG + BATCH - 1
+LAG_NORMALISE = LAG_TURN_LOG + 1
 LAG_ATTEND = LAG_NORMALISE + 1
 LAG_PROJECT = LAG_ATTEND + 1
 
@@ -111,7 +111,7 @@ def tile_attention2_pa_t_kernel(tc, q, k, v, w_proj, out):
             nc.scalar.copy(out=turned, in_=tr_ps[:])
 
         def turn_w(g):
-            w_ps = psum.tile([P, PACK, P], BF16, tag="o")
+            w_ps = psum.tile([P, PACK, P], BF16, tag=f"out{g % 2}")
             for t in range(PACK):
                 nc.tensor.transpose(out=w_ps[:, t, :], in_=w_rows[:, g, t * P : (t + 1) * P], identity=ident[:])
             nc.scalar.copy(out=w_grouped[:, g * P : (g + 1) * P, :], in_=w_ps[:].rearrange("p t c -> p c t"))
@@ -120,7 +120,11 @@ def tile_attention2_pa_t_kernel(tc, q, k, v, w_proj, out):
             if h == 0:
                 v_grouped = two.tile([P, HEADS, HEAD_DIM, PACK], BF16, align_bytes=64)
                 v_grouped_of[b] = v_grouped
-            nc.vector.tensor_copy(out=v_grouped_of[b][:, h], in_=v_rows_of[b][:, h].rearrange("p t d -> p d t"))
+            engine = nc.vector if b < 2 else nc.gpsimd
+            engine.tensor_scalar(
+                out=v_grouped_of[b][:, h], in0=v_rows_of[b][:, h].rearrange("p t d -> p d t"),
+                scalar1=1.0, scalar2=0.0, op0=ALU.mult, op1=ALU.add,
+            )
 
         def quantise_v(b, h):
             if h == 0:
@@ -138,9 +142,9 @@ def tile_attention2_pa_t_kernel(tc, q, k, v, w_proj, out):
                 nc.tensor.matmul(out=s_ps[:, t, :], lhsT=kT[:, h, t, :], rhs=qT[:, h, c % TILES, :], start=True, stop=True)
             s_of[c, h] = s_ps[:].rearrange("p t n -> p n t")
 
-        def copy_first(c):
-            first = two.tile([P, P, PACK], F32)
-            nc.vector.tensor_copy(out=first[:], in_=s_of[c, 0])
+        def copy_first(c, copy):
+            first = three.tile([P, P, PACK], F32)
+            copy(out=first[:], in_=s_of[c, 0])
             first_of[c] = first
 
         def maximum(c, h):
@@ -180,8 +184,8 @@ def tile_attention2_pa_t_kernel(tc, q, k, v, w_proj, out):
         def logarithm(c):
             nc.scalar.activation(out=sums_of[c][:], in_=sums_of[c][:], func=ACT.Ln)
 
-        def turn_log(c):
-            log_ps = psum.tile([P, PACK, P], F32, tag="o")
+        def turn_log(c, bank):
+            log_ps = psum.tile([P, PACK, P], F32, tag=bank)
             for i in range(PACK):
                 nc.tensor.transpose(out=log_ps[:, i, :], in_=sums_of[c][:, i * P : (i + 1) * P], identity=ident_f32[:])
             inverse = two.tile([P, PACK, P], F32)
@@ -191,8 +195,8 @@ def tile_attention2_pa_t_kernel(tc, q, k, v, w_proj, out):
             log_ps, inverse = inverse_of[c]
             nc.scalar.activation(out=inverse[:], in_=log_ps[:], func=ACT.Exp, scale=-1.0)
 
-        def turn_inverse(c):
-            inv_ps = psum.tile([P, PACK, P], F32, tag="inv")
+        def turn_inverse(c, bank):
+            inv_ps = psum.tile([P, PACK, P], F32, tag=bank)
             for i in range(PACK):
                 nc.tensor.transpose(out=inv_ps[:, i, :], in_=inverse_of[c][1][:, i, :], identity=ident_f32[:])
             inv_ps_of[c] = inv_ps
@@ -235,11 +239,11 @@ def tile_attention2_pa_t_kernel(tc, q, k, v, w_proj, out):
             mx_pass(nc, out_ps[:], o_codes[:], o_scales[:], w_codes[:, cols], w_scales[:, cols])
             out_ps_of[c, half] = out_ps
 
-        def copy_out(c, half):
+        def copy_out(c, half, copy):
             if half == 0:
                 out_rows = three.tile([P, OUT_CH], F32)
                 out_rows_of[c] = out_rows
-            nc.scalar.copy(out=out_rows_of[c][:, half * BANK : (half + 1) * BANK], in_=out_ps_of[c, half][:])
+            copy(out=out_rows_of[c][:, half * BANK : (half + 1) * BANK], in_=out_ps_of[c, half][:])
 
         def store(c):
             nc.sync.dma_start(out=out[c // TILES].rearrange("(p j) c -> p j c", j=TILES)[:, c % TILES, :], in_=out_rows_of[c][:])
@@ -259,81 +263,97 @@ def tile_attention2_pa_t_kernel(tc, q, k, v, w_proj, out):
         exps = [(c, h) for c in range(CHUNKS) for h in (1, 2, 3, 0)]
         adds = [(c, i) for c in range(CHUNKS) for i in range(3)]
         done = added = 0
+        firsts = list(range(0, CHUNKS, BATCH))
+        batches = {x + LAG_TURN_LOG - (1 if x >= CHUNKS - BATCH else 0): range(x, y) for x, y in zip(firsts, firsts[1:] + [CHUNKS])}
         for step in range(CHUNKS + LAG_PROJECT + 1):
             b, j = step // TILES, step % TILES
-            c_inv, c_norm, c_att, c_proj = step - LAG_INVERT, step - LAG_NORMALISE, step - LAG_ATTEND, step - LAG_PROJECT
-            last = step - LAG_LOG
-            logs = list(range(last - BATCH + 1, last + 1)) if ok(last) and last % BATCH == BATCH - 1 else []
-            quota = (0, 5, 5, 6)[(step - LAG_LOG + 1) % BATCH] if step >= LAG_LOG - 1 else 4
+            tail = step >= CHUNKS
+            c_log, c_norm, c_att, c_proj = step - LAG_TURN_LOG, step - LAG_NORMALISE, step - LAG_ATTEND, step - LAG_PROJECT
+            phase = c_log % BATCH
+            logs = list(batches.get(step, ()))
+            quota = 8 if tail else (0, 4, 6, 6)[phase] if step >= BATCH - 1 else 4
             todo = [x for x in exps[done : done + quota] if x[0] < step]
             done_before = done
             done += len(todo)
-            groups = (todo[:2], todo[2:])
-
-            def exp_group(i):
-                for c, h in groups[i]:
-                    exponential(c, h)
+            early = 4
 
             if j == 0 and b + 2 < FRAMES:
                 load_qk(b + 2)
             if j == 0 and b + 1 < FRAMES:
                 load_v(b + 1)
             if ok(step):
-                copy_first(step)
+                copy_first(step, nc.vector.tensor_copy)
             if step < len(turns):
                 turn(*turns[step], "s0")
+            if ok(c_norm) and step <= CHUNKS:
+                invert(c_norm)
+            for c in logs[:1]:
+                logarithm(c)
             if step < len(turns):
                 turned_copy(*turns[step])
+            for c in logs[1:]:
+                logarithm(c)
+            if tail and ok(c_log):
+                turn_log(c_log, ("s1", "s2")[step % 2])
+            if tail and ok(c_norm):
+                turn_inverse(c_norm, ("s3", "inv")[step % 2])
+            if tail and ok(c_log):
+                invert(c_log)
+            for c, h in todo[:early]:
+                exponential(c, h)
             if ok(c_att):
-                normalise(c_att, 2)
+                normalise(c_att, 1)
             if ok(step):
                 maximum(step, 1)
             if ok(c_att):
-                normalise(c_att, 3)
-            if ok(c_norm):
-                turn_inverse(c_norm)
+                normalise(c_att, 2)
             if ok(step):
                 maximum(step, 2)
             if ok(c_att):
-                attend(c_att)
-            if ok(c_proj):
+                normalise(c_att, 3)
+            if ok(step):
+                maximum(step, 3)
+            if ok(c_proj) and not tail:
                 quantise_o(c_proj)
                 project(c_proj, 0)
                 project(c_proj, 1)
+            if 0 < step <= W_GROUPS // 2:
+                part = slice((step - 1) * 2 * P, step * 2 * P)
+                quantise(nc, w_codes[:, part], w_scales[:, part], w_grouped[:, part].rearrange("p c t -> p (c t)"))
             if ok(step - 1):
                 quantise_v((step - 1) // TILES, (step - 1) % TILES)
-            if b < FRAMES:
+            if b < 2:
                 group_v(b, j)
-            if step < W_GROUPS // 2:
-                turn_w(2 * step)
-                turn_w(2 * step + 1)
-            if step == W_GROUPS // 2:
-                quantise(nc, w_codes[:], w_scales[:], w_grouped[:].rearrange("p c t -> p (c t)"))
+            if ok(c_norm) and not tail:
+                turn_inverse(c_norm, "inv")
+            if ok(c_att):
+                attend(c_att)
+            if tail and ok(c_att):
+                regroup_o(c_att)
+            if ok(c_proj) and tail:
+                quantise_o(c_proj)
+                project(c_proj, 0)
+                project(c_proj, 1)
             if ok(step):
-                maximum(step, 3)
                 subtract(step, 0)
-            for c, i in adds[added : added + 3]:
+            for c, i in adds[added : added + (8 if tail else 3)]:
                 if exps.index((c, 2 if i == 0 else 0)) < done_before:
                     if i < 2:
                         add_pair(c, i, (1, 3)[i], (2, 0)[i])
                     else:
                         add_pairs(c)
                     added += 1
-            if ok(c_norm):
-                normalise(c_norm, 0)
-            if ok(c_att):
+            if 2 <= b < FRAMES:
+                group_v(b, j)
+            if ok(c_proj):
+                copy_out(c_proj, 0, nc.scalar.copy)
+            if ok(c_att) and not tail:
                 regroup_o(c_att)
             if ok(c_proj):
-                copy_out(c_proj, 0)
-                copy_out(c_proj, 1)
+                copy_out(c_proj, 1, nc.scalar.copy)
                 store(c_proj)
-            if ok(c_inv):
-                turn_log(c_inv)
-                invert(c_inv)
-            exp_group(0)
-            exp_group(1)
-            for c in logs:
-                logarithm(c)
+            for c, h in todo[early:]:
+                exponential(c, h)
             if step + 1 < CHUNKS:
                 scores(step + 1, 0)
             for h in range(1, HEADS):
@@ -341,5 +361,10 @@ def tile_attention2_pa_t_kernel(tc, q, k, v, w_proj, out):
                     subtract(step, h)
                 if step + 1 < CHUNKS:
                     scores(step + 1, h)
+            if step < W_GROUPS // 2:
+                turn_w(2 * step)
+                turn_w(2 * step + 1)
             if ok(c_norm):
-                normalise(c_norm, 1)
+                normalise(c_norm, 0)
+            if ok(c_log) and not tail:
+                turn_log(c_log, "o")

@@ -23,7 +23,7 @@ W_GROUPS = OUT_CH // P
 
 BATCH = TILES
 
-LAG_LOG = 4
+LAG_LOG = 3
 LAG_TURN_LOG = LAG_LOG + BATCH - 1
 LAG_NORMALISE = LAG_TURN_LOG + 1
 LAG_ATTEND = LAG_NORMALISE + 1
@@ -117,12 +117,10 @@ def tile_attention2_pa_t_kernel(tc, q, k, v, w_proj, out):
             nc.scalar.copy(out=w_grouped[:, g * P : (g + 1) * P, :], in_=w_ps[:].rearrange("p t c -> p c t"))
 
         def group_v(b, h):
-            if h == 0:
-                v_grouped = two.tile([P, HEADS, HEAD_DIM, PACK], BF16, align_bytes=64)
-                v_grouped_of[b] = v_grouped
-            engine = nc.vector if b < 2 else nc.gpsimd
-            engine.tensor_scalar(
-                out=v_grouped_of[b][:, h], in0=v_rows_of[b][:, h].rearrange("p t d -> p d t"),
+            v_grouped = const.tile([P, HEAD_DIM, PACK], BF16, align_bytes=64)
+            v_grouped_of[b, h] = v_grouped
+            nc.gpsimd.tensor_scalar(
+                out=v_grouped[:], in0=v_rows_of[b][:, h].rearrange("p t d -> p d t"),
                 scalar1=1.0, scalar2=0.0, op0=ALU.mult, op1=ALU.add,
             )
 
@@ -133,7 +131,7 @@ def tile_attention2_pa_t_kernel(tc, q, k, v, w_proj, out):
                 v_mx_of[b] = (v_codes, v_scales)
             v_codes, v_scales = v_mx_of[b]
             cols = slice(h * HEAD_DIM, (h + 1) * HEAD_DIM)
-            quantise(nc, v_codes[:, cols], v_scales[:, cols], v_grouped_of[b][:, h].rearrange("p d t -> p (d t)"))
+            quantise(nc, v_codes[:, cols], v_scales[:, cols], v_grouped_of[b, h][:].rearrange("p d t -> p (d t)"))
 
         def scores(c, h):
             kT, qT = turned_of[c // TILES]
@@ -264,7 +262,7 @@ def tile_attention2_pa_t_kernel(tc, q, k, v, w_proj, out):
         adds = [(c, i) for c in range(CHUNKS) for i in range(3)]
         done = added = 0
         firsts = list(range(0, CHUNKS, BATCH))
-        batches = {x + LAG_TURN_LOG - (1 if x >= CHUNKS - BATCH else 0): range(x, y) for x, y in zip(firsts, firsts[1:] + [CHUNKS])}
+        batches = {x + LAG_TURN_LOG - (0 if x >= CHUNKS - BATCH else 0): range(x, y) for x, y in zip(firsts, firsts[1:] + [CHUNKS])}
         for step in range(CHUNKS + LAG_PROJECT + 1):
             b, j = step // TILES, step % TILES
             tail = step >= CHUNKS
@@ -291,8 +289,9 @@ def tile_attention2_pa_t_kernel(tc, q, k, v, w_proj, out):
                 logarithm(c)
             if step < len(turns):
                 turned_copy(*turns[step])
-            for c in logs[1:]:
-                logarithm(c)
+            if tail:
+                for c in logs[1:]:
+                    logarithm(c)
             if tail and ok(c_log):
                 turn_log(c_log, ("s1", "s2")[step % 2])
             if tail and ok(c_norm):
@@ -307,13 +306,16 @@ def tile_attention2_pa_t_kernel(tc, q, k, v, w_proj, out):
                 maximum(step, 1)
             if ok(c_att):
                 normalise(c_att, 2)
+                normalise(c_att, 3)
+            if ok(c_norm) and not tail:
+                turn_inverse(c_norm, "inv")
             if ok(step):
                 maximum(step, 2)
             if ok(c_att):
-                normalise(c_att, 3)
-            if ok(step):
-                maximum(step, 3)
-            if ok(c_proj) and not tail:
+                attend(c_att)
+            if tail and ok(c_att):
+                regroup_o(c_att)
+            if ok(c_proj):
                 quantise_o(c_proj)
                 project(c_proj, 0)
                 project(c_proj, 1)
@@ -322,34 +324,30 @@ def tile_attention2_pa_t_kernel(tc, q, k, v, w_proj, out):
                 quantise(nc, w_codes[:, part], w_scales[:, part], w_grouped[:, part].rearrange("p c t -> p (c t)"))
             if ok(step - 1):
                 quantise_v((step - 1) // TILES, (step - 1) % TILES)
-            if b < 2:
+            if b < FRAMES:
                 group_v(b, j)
-            if ok(c_norm) and not tail:
-                turn_inverse(c_norm, "inv")
-            if ok(c_att):
-                attend(c_att)
-            if tail and ok(c_att):
-                regroup_o(c_att)
-            if ok(c_proj) and tail:
-                quantise_o(c_proj)
-                project(c_proj, 0)
-                project(c_proj, 1)
-            if ok(step):
-                subtract(step, 0)
             for c, i in adds[added : added + (8 if tail else 3)]:
-                if exps.index((c, 2 if i == 0 else 0)) < done_before:
+                if exps.index((c, 2 if i == 0 else 0)) < done_before + len(todo[:early]):
                     if i < 2:
                         add_pair(c, i, (1, 3)[i], (2, 0)[i])
                     else:
                         add_pairs(c)
                     added += 1
-            if 2 <= b < FRAMES:
-                group_v(b, j)
-            if ok(c_proj):
-                copy_out(c_proj, 0, nc.scalar.copy)
+            if ok(step):
+                maximum(step, 3)
+                subtract(step, 0)
+            if ok(c_norm):
+                normalise(c_norm, 0)
+            if not tail:
+                for c in logs[1:2]:
+                    logarithm(c)
             if ok(c_att) and not tail:
                 regroup_o(c_att)
+            if not tail:
+                for c in logs[2:]:
+                    logarithm(c)
             if ok(c_proj):
+                copy_out(c_proj, 0, nc.scalar.copy)
                 copy_out(c_proj, 1, nc.scalar.copy)
                 store(c_proj)
             for c, h in todo[early:]:
@@ -364,7 +362,5 @@ def tile_attention2_pa_t_kernel(tc, q, k, v, w_proj, out):
             if step < W_GROUPS // 2:
                 turn_w(2 * step)
                 turn_w(2 * step + 1)
-            if ok(c_norm):
-                normalise(c_norm, 0)
             if ok(c_log) and not tail:
                 turn_log(c_log, "o")

@@ -23,11 +23,12 @@ W_GROUPS = OUT_CH // P
 
 BATCH = TILES
 
-LAG_LOG = 3
-LAG_TURN_LOG = LAG_LOG + BATCH - 1
-LAG_NORMALISE = LAG_TURN_LOG + 1
+LAG_LOG = BATCH + 2
+LAG_NORMALISE = LAG_LOG + 1
 LAG_ATTEND = LAG_NORMALISE + 1
 LAG_PROJECT = LAG_ATTEND + 1
+
+ORDER = (1, 2, 3, 0)
 
 FLOPS = 2 * FRAMES * HEADS * TOKENS * TOKENS * HEAD_DIM * 2 + 2 * FRAMES * TOKENS * CHANNELS * OUT_CH
 
@@ -106,9 +107,9 @@ def tile_attention2_pa_t_kernel(tc, q, k, v, w_proj, out):
                     nc.tensor.transpose(out=tr_ps[:, i, j, :], in_=rows[:, first + i, j, :], identity=ident[:])
             tr_ps_of[b, quarter] = (turned[:, first : first + 2, :, :], tr_ps)
 
-        def turned_copy(b, quarter):
+        def turned_copy(b, quarter, copy):
             turned, tr_ps = tr_ps_of[b, quarter]
-            nc.scalar.copy(out=turned, in_=tr_ps[:])
+            copy(out=turned, in_=tr_ps[:])
 
         def turn_w(g):
             w_ps = psum.tile([P, PACK, P], BF16, tag=f"out{g % 2}")
@@ -141,7 +142,7 @@ def tile_attention2_pa_t_kernel(tc, q, k, v, w_proj, out):
             s_of[c, h] = s_ps[:].rearrange("p t n -> p n t")
 
         def copy_first(c, copy):
-            first = three.tile([P, P, PACK], F32)
+            first = two.tile([P, P, PACK], F32)
             copy(out=first[:], in_=s_of[c, 0])
             first_of[c] = first
 
@@ -151,33 +152,35 @@ def tile_attention2_pa_t_kernel(tc, q, k, v, w_proj, out):
             nc.vector.tensor_tensor(out=top[:], in0=s_of[c, h], in1=before[:], op=ALU.max)
             top_of[c] = top
 
-        def subtract(c, h):
-            shifted = three.tile([P, P, PACK], F32, tag=f"shifted{h}")
-            if h == 0:
-                nc.gpsimd.tensor_tensor(out=shifted[:], in0=first_of[c][:], in1=top_of[c][:], op=ALU.subtract)
-            else:
-                nc.vector.tensor_tensor(out=shifted[:], in0=s_of[c, h], in1=top_of[c][:], op=ALU.subtract)
-            shifted_of[c, h] = shifted
+        def subtract(c, h, in_psum=False):
+            if c not in shifted_of:
+                shifted = three.tile([P, HEADS, P, PACK], F32)
+                shifted_of[c] = shifted
+            engine = nc.gpsimd if h == 0 and not in_psum else nc.vector
+            scores_h = first_of[c][:] if h == 0 and not in_psum else s_of[c, h]
+            engine.tensor_tensor(out=shifted_of[c][:, ORDER.index(h)], in0=scores_h, in1=top_of[c][:], op=ALU.subtract)
 
-        def exponential(c, h):
-            if c not in e_of:
+        def exponential(c, half):
+            if half == 0:
                 e = deep.tile([P, HEADS, P, PACK], F32, align_bytes=64, tag="e")
                 e_of[c] = e
-            nc.scalar.activation(out=e_of[c][:, h], in_=shifted_of[c, h][:], func=ACT.Exp, scale=SCALE)
+            pair = slice(2 * half, 2 * half + 2)
+            nc.scalar.activation(out=e_of[c][:, pair], in_=shifted_of[c][:, pair], func=ACT.Exp, scale=SCALE)
 
-        def add_pair(c, i, a, b):
+        def add(c, i):
             if i == 0:
-                pair = const.tile([P, 2, P, PACK], F32)
-                sums_of[c] = pair
-            nc.gpsimd.tensor_tensor(out=sums_of[c][:, i], in0=e_of[c][:, a], in1=e_of[c][:, b], op=ALU.add)
-
-        def add_pairs(c):
-            total = deep.tile([P, P * PACK], F32)
-            pair = sums_of[c]
-            nc.gpsimd.tensor_tensor(
-                out=total[:], in0=pair[:, 0].rearrange("p n t -> p (n t)"), in1=pair[:, 1].rearrange("p n t -> p (n t)"), op=ALU.add
-            )
-            sums_of[c] = total
+                pair_sums = const.tile([P, 2, P, PACK], F32)
+                sums_of[c] = pair_sums
+            if i < 2:
+                nc.gpsimd.tensor_tensor(out=sums_of[c][:, i], in0=e_of[c][:, 2 * i], in1=e_of[c][:, 2 * i + 1], op=ALU.add)
+            else:
+                total = deep.tile([P, P * PACK], F32)
+                pair_sums = sums_of[c]
+                nc.gpsimd.tensor_tensor(
+                    out=total[:], in0=pair_sums[:, 0].rearrange("p n t -> p (n t)"), in1=pair_sums[:, 1].rearrange("p n t -> p (n t)"),
+                    op=ALU.add,
+                )
+                sums_of[c] = total
 
         def logarithm(c):
             nc.scalar.activation(out=sums_of[c][:], in_=sums_of[c][:], func=ACT.Ln)
@@ -199,13 +202,15 @@ def tile_attention2_pa_t_kernel(tc, q, k, v, w_proj, out):
                 nc.tensor.transpose(out=inv_ps[:, i, :], in_=inverse_of[c][1][:, i, :], identity=ident_f32[:])
             inv_ps_of[c] = inv_ps
 
-        def normalise(c, h):
-            if h == 0:
+        def normalise(c, slots):
+            if slots[0] == 0:
                 attn = three.tile([P, HEADS, P * PACK], BF16, align_bytes=64)
                 attn_of[c] = attn
+            count = len(slots)
+            part = slice(slots[0], slots[0] + count)
             nc.vector.tensor_tensor(
-                out=attn_of[c][:, h], in0=e_of[c][:, h].rearrange("p n t -> p (n t)"),
-                in1=inv_ps_of[c][:].rearrange("p i n -> p (i n)"), op=ALU.mult,
+                out=attn_of[c][:, part], in0=e_of[c][:, part].rearrange("p h n t -> p h (n t)"),
+                in1=inv_ps_of[c][:].rearrange("p i n -> p (i n)").unsqueeze(1).to_broadcast([P, count, P * PACK]), op=ALU.mult,
             )
 
         def attend(c):
@@ -214,9 +219,9 @@ def tile_attention2_pa_t_kernel(tc, q, k, v, w_proj, out):
             quantise(nc, attn_codes[:], attn_scales[:], attn_of[c][:].rearrange("p h m -> p (h m)"))
             v_codes, v_scales = v_mx_of[c // TILES]
             o_ps = psum.tile([P, HEADS, P], F32, tag="o")
-            for h in range(HEADS):
-                cols = slice(h * P, (h + 1) * P)
-                mx_pass(nc, o_ps[:, h, :], v_codes[:, cols], v_scales[:, cols], attn_codes[:, cols], attn_scales[:, cols])
+            for slot, h in enumerate(ORDER):
+                rhs, lhs = slice(slot * P, (slot + 1) * P), slice(h * P, (h + 1) * P)
+                mx_pass(nc, o_ps[:, h, :], v_codes[:, lhs], v_scales[:, lhs], attn_codes[:, rhs], attn_scales[:, rhs])
             o_ps_of[c] = o_ps
 
         def regroup_o(c):
@@ -224,29 +229,24 @@ def tile_attention2_pa_t_kernel(tc, q, k, v, w_proj, out):
             nc.scalar.copy(out=o_grouped[:], in_=o_ps_of[c][:].rearrange("p h n -> p n h"))
             o_ps_of[c] = o_grouped
 
-        def quantise_o(c):
+        def project(c):
             o_codes = two.tile([P, P], U32, align_bytes=64)
             o_scales = two.tile([P, P], U8, align_bytes=64)
             quantise(nc, o_codes[:], o_scales[:], o_ps_of[c][:].rearrange("p n h -> p (n h)"))
-            o_mx_of[c] = (o_codes, o_scales)
+            for half in range(OUT_CH // BANK):
+                cols = slice(half * BANK, (half + 1) * BANK)
+                out_ps = psum.tile([P, BANK], F32, tag=f"out{half}")
+                mx_pass(nc, out_ps[:], o_codes[:], o_scales[:], w_codes[:, cols], w_scales[:, cols])
+                out_ps_of[c, half] = out_ps
 
-        def project(c, half):
-            o_codes, o_scales = o_mx_of[c]
-            cols = slice(half * BANK, (half + 1) * BANK)
-            out_ps = psum.tile([P, BANK], F32, tag=f"out{half}")
-            mx_pass(nc, out_ps[:], o_codes[:], o_scales[:], w_codes[:, cols], w_scales[:, cols])
-            out_ps_of[c, half] = out_ps
-
-        def copy_out(c, half, copy):
-            if half == 0:
-                out_rows = three.tile([P, OUT_CH], F32)
-                out_rows_of[c] = out_rows
-            copy(out=out_rows_of[c][:, half * BANK : (half + 1) * BANK], in_=out_ps_of[c, half][:])
-
-        def store(c):
-            nc.sync.dma_start(out=out[c // TILES].rearrange("(p j) c -> p j c", j=TILES)[:, c % TILES, :], in_=out_rows_of[c][:])
+        def store(c, copies):
+            out_rows = three.tile([P, OUT_CH], F32)
+            for half in range(OUT_CH // BANK):
+                copies[half](out=out_rows[:, half * BANK : (half + 1) * BANK], in_=out_ps_of[c, half][:])
+            nc.sync.dma_start(out=out[c // TILES].rearrange("(p j) c -> p j c", j=TILES)[:, c % TILES, :], in_=out_rows[:])
 
         turns = [(b, quarter) for b in range(1, FRAMES) for quarter in range(4)]
+        vector_copy, scalar_copy = nc.vector.tensor_copy, nc.scalar.copy
 
         load_qk(0)
         load_v(0)
@@ -254,33 +254,32 @@ def tile_attention2_pa_t_kernel(tc, q, k, v, w_proj, out):
         load_qk(1)
         for quarter in range(4):
             turn(0, quarter, f"s{quarter}")
-            turned_copy(0, quarter)
+            turned_copy(0, quarter, scalar_copy)
         for h in range(HEADS):
             scores(0, h)
 
-        exps = [(c, h) for c in range(CHUNKS) for h in (1, 2, 3, 0)]
+        exps = [(c, half) for c in range(CHUNKS) for half in range(2)]
         adds = [(c, i) for c in range(CHUNKS) for i in range(3)]
         done = added = 0
-        firsts = list(range(0, CHUNKS, BATCH))
-        batches = {x + LAG_TURN_LOG - (0 if x >= CHUNKS - BATCH else 0): range(x, y) for x, y in zip(firsts, firsts[1:] + [CHUNKS])}
         for step in range(CHUNKS + LAG_PROJECT + 1):
             b, j = step // TILES, step % TILES
             tail = step >= CHUNKS
-            c_log, c_norm, c_att, c_proj = step - LAG_TURN_LOG, step - LAG_NORMALISE, step - LAG_ATTEND, step - LAG_PROJECT
+            c_log, c_norm, c_att, c_proj = step - LAG_LOG, step - LAG_NORMALISE, step - LAG_ATTEND, step - LAG_PROJECT
             phase = c_log % BATCH
-            logs = list(batches.get(step, ()))
-            quota = 8 if tail else (0, 4, 6, 6)[phase] if step >= BATCH - 1 else 4
+            logs = list(range(c_log, c_log + BATCH)) if ok(c_log) and phase == 0 else []
+            quota = 4 if tail else (0, 2, 3, 3)[phase] if step >= BATCH - 1 else 2
             todo = [x for x in exps[done : done + quota] if x[0] < step]
-            done_before = done
+            early = todo[: 2]
+            done_early = done + len(early)
             done += len(todo)
-            early = 4
+            s_next = phase == 2 and step + 1 < CHUNKS
 
             if j == 0 and b + 2 < FRAMES:
                 load_qk(b + 2)
             if j == 0 and b + 1 < FRAMES:
                 load_v(b + 1)
-            if ok(step):
-                copy_first(step, nc.vector.tensor_copy)
+            if ok(step) and step not in first_of:
+                copy_first(step, vector_copy)
             if step < len(turns):
                 turn(*turns[step], "s0")
             if ok(c_norm) and step <= CHUNKS:
@@ -288,72 +287,67 @@ def tile_attention2_pa_t_kernel(tc, q, k, v, w_proj, out):
             for c in logs[:1]:
                 logarithm(c)
             if step < len(turns):
-                turned_copy(*turns[step])
+                turned_copy(*turns[step], scalar_copy)
             if tail:
                 for c in logs[1:]:
                     logarithm(c)
-            if tail and ok(c_log):
-                turn_log(c_log, ("s1", "s2")[step % 2])
-            if tail and ok(c_norm):
-                turn_inverse(c_norm, ("s3", "inv")[step % 2])
-            if tail and ok(c_log):
-                invert(c_log)
-            for c, h in todo[:early]:
-                exponential(c, h)
+                if ok(c_log):
+                    turn_log(c_log, ("s1", "s2")[step % 2])
+                if ok(c_norm):
+                    turn_inverse(c_norm, ("s3", "inv")[step % 2])
+                if ok(c_log):
+                    invert(c_log)
+            for c, half in early:
+                exponential(c, half)
             if ok(c_att):
-                normalise(c_att, 1)
+                normalise(c_att, (1,))
             if ok(step):
                 maximum(step, 1)
             if ok(c_att):
-                normalise(c_att, 2)
-                normalise(c_att, 3)
+                normalise(c_att, (2, 3))
             if ok(c_norm) and not tail:
                 turn_inverse(c_norm, "inv")
             if ok(step):
                 maximum(step, 2)
+            if CHUNKS < step <= CHUNKS + 2:
+                store(c_proj - 1, (vector_copy, vector_copy))
             if ok(c_att):
                 attend(c_att)
-            if tail and ok(c_att):
-                regroup_o(c_att)
+                if tail:
+                    regroup_o(c_att)
             if ok(c_proj):
-                quantise_o(c_proj)
-                project(c_proj, 0)
-                project(c_proj, 1)
+                project(c_proj)
+            if ok(step - 1):
+                quantise_v((step - 1) // TILES, (step - 1) % TILES)
             if 0 < step <= W_GROUPS // 2:
                 part = slice((step - 1) * 2 * P, step * 2 * P)
                 quantise(nc, w_codes[:, part], w_scales[:, part], w_grouped[:, part].rearrange("p c t -> p (c t)"))
-            if ok(step - 1):
-                quantise_v((step - 1) // TILES, (step - 1) % TILES)
             if b < FRAMES:
                 group_v(b, j)
             for c, i in adds[added : added + (8 if tail else 3)]:
-                if exps.index((c, 2 if i == 0 else 0)) < done_before + len(todo[:early]):
-                    if i < 2:
-                        add_pair(c, i, (1, 3)[i], (2, 0)[i])
-                    else:
-                        add_pairs(c)
+                if exps.index((c, min(i, 1))) < done_early:
+                    add(c, i)
                     added += 1
             if ok(step):
                 maximum(step, 3)
                 subtract(step, 0)
             if ok(c_norm):
-                normalise(c_norm, 0)
+                normalise(c_norm, (0,))
             if not tail:
                 for c in logs[1:2]:
                     logarithm(c)
-            if ok(c_att) and not tail:
-                regroup_o(c_att)
-            if not tail:
+                if ok(c_att):
+                    regroup_o(c_att)
                 for c in logs[2:]:
                     logarithm(c)
-            if ok(c_proj):
-                copy_out(c_proj, 0, nc.scalar.copy)
-                copy_out(c_proj, 1, nc.scalar.copy)
-                store(c_proj)
-            for c, h in todo[early:]:
-                exponential(c, h)
             if step + 1 < CHUNKS:
                 scores(step + 1, 0)
+                if s_next:
+                    copy_first(step + 1, scalar_copy)
+            if ok(c_proj) and not CHUNKS <= step < CHUNKS + 2:
+                store(c_proj, (scalar_copy, scalar_copy))
+            for c, half in todo[len(early) :]:
+                exponential(c, half)
             for h in range(1, HEADS):
                 if ok(step):
                     subtract(step, h)

@@ -56,6 +56,7 @@ def tile_attention2_pa_t_kernel(tc, q, k, v, w_proj, out):
         const = stack.enter_context(tc.tile_pool(name="const", bufs=1))
         two = stack.enter_context(tc.tile_pool(name="two", bufs=2))
         three = stack.enter_context(tc.tile_pool(name="three", bufs=3))
+        four = stack.enter_context(tc.tile_pool(name="four", bufs=4))
         deep = stack.enter_context(tc.tile_pool(name="deep", bufs=LAG_NORMALISE + 1))
         psum = stack.enter_context(tc.psum_pool(name="psum", bufs=1))
 
@@ -111,16 +112,25 @@ def tile_attention2_pa_t_kernel(tc, q, k, v, w_proj, out):
             turned, tr_ps = tr_ps_of[b, quarter]
             copy(out=turned, in_=tr_ps[:])
 
+        def turn_first_queries(first, tiles, bank, copy):
+            q_rows, qT = rows_of[0][1], turned_of[0][1]
+            heads, count = slice(first, first + 2), tiles.stop - tiles.start
+            tr_ps = psum.tile([P, 2, count, P], BF16, tag=bank)
+            for i in range(2):
+                for j in range(count):
+                    nc.tensor.transpose(out=tr_ps[:, i, j, :], in_=q_rows[:, first + i, tiles.start + j, :], identity=ident[:])
+            copy(out=qT[:, heads, tiles, :], in_=tr_ps[:])
+
         def turn_w(g):
             w_ps = psum.tile([P, PACK, P], BF16, tag=f"out{g % 2}")
             for t in range(PACK):
                 nc.tensor.transpose(out=w_ps[:, t, :], in_=w_rows[:, g, t * P : (t + 1) * P], identity=ident[:])
             nc.scalar.copy(out=w_grouped[:, g * P : (g + 1) * P, :], in_=w_ps[:].rearrange("p t c -> p c t"))
 
-        def group_v(b, h):
+        def group_v(b, h, engine):
             v_grouped = const.tile([P, HEAD_DIM, PACK], BF16, align_bytes=64)
             v_grouped_of[b, h] = v_grouped
-            nc.gpsimd.tensor_scalar(
+            engine.tensor_scalar(
                 out=v_grouped[:], in0=v_rows_of[b][:, h].rearrange("p t d -> p d t"),
                 scalar1=1.0, scalar2=0.0, op0=ALU.mult, op1=ALU.add,
             )
@@ -142,7 +152,7 @@ def tile_attention2_pa_t_kernel(tc, q, k, v, w_proj, out):
             s_of[c, h] = s_ps[:].rearrange("p t n -> p n t")
 
         def copy_first(c, copy):
-            first = two.tile([P, P, PACK], F32)
+            first = four.tile([P, P, PACK], F32)
             copy(out=first[:], in_=s_of[c, 0])
             first_of[c] = first
 
@@ -239,6 +249,10 @@ def tile_attention2_pa_t_kernel(tc, q, k, v, w_proj, out):
                 mx_pass(nc, out_ps[:], o_codes[:], o_scales[:], w_codes[:, cols], w_scales[:, cols])
                 out_ps_of[c, half] = out_ps
 
+        def keep_warm(half):
+            idle_ps = psum.tile([P, BANK], F32, tag=f"out{half}")
+            mx_pass(nc, idle_ps[:], w_codes[:, :P], w_scales[:, :P], w_codes[:, BANK:], w_scales[:, BANK:])
+
         def store(c, copies):
             out_rows = three.tile([P, OUT_CH], F32)
             for half in range(OUT_CH // BANK):
@@ -252,11 +266,14 @@ def tile_attention2_pa_t_kernel(tc, q, k, v, w_proj, out):
         load_v(0)
         nc.sync.dma_start(out=w_rows[:], in_=w_proj.rearrange("(g p) c -> p g c", p=P))
         load_qk(1)
-        for quarter in range(4):
+        for quarter in (0, 2):
             turn(0, quarter, f"s{quarter}")
             turned_copy(0, quarter, scalar_copy)
+            turn_first_queries(quarter, slice(0, 1), f"s{quarter + 1}", vector_copy)
         for h in range(HEADS):
             scores(0, h)
+        for quarter in (0, 2):
+            turn_first_queries(quarter, slice(1, TILES), f"out{quarter // 2}", scalar_copy)
 
         exps = [(c, half) for c in range(CHUNKS) for half in range(2)]
         adds = [(c, i) for c in range(CHUNKS) for i in range(3)]
@@ -269,10 +286,12 @@ def tile_attention2_pa_t_kernel(tc, q, k, v, w_proj, out):
             logs = list(range(c_log, c_log + BATCH)) if ok(c_log) and phase == 0 else []
             quota = 4 if tail else (0, 2, 3, 3)[phase] if step >= BATCH - 1 else 2
             todo = [x for x in exps[done : done + quota] if x[0] < step]
-            early = todo[: 2]
+            early = todo[: 3]
             done_early = done + len(early)
             done += len(todo)
-            s_next = phase == 2 and step + 1 < CHUNKS
+            s_next = (phase == 2) and step + 1 < CHUNKS
+            late = phase == 1
+            shared = (False) and not tail
 
             if j == 0 and b + 2 < FRAMES:
                 load_qk(b + 2)
@@ -307,6 +326,8 @@ def tile_attention2_pa_t_kernel(tc, q, k, v, w_proj, out):
                 normalise(c_att, (2, 3))
             if ok(c_norm) and not tail:
                 turn_inverse(c_norm, "inv")
+            if 6 <= step < CHUNKS:
+                keep_warm(0)
             if ok(step):
                 maximum(step, 2)
             if CHUNKS < step <= CHUNKS + 2:
@@ -315,6 +336,10 @@ def tile_attention2_pa_t_kernel(tc, q, k, v, w_proj, out):
                 attend(c_att)
                 if tail:
                     regroup_o(c_att)
+            if step + 1 < CHUNKS:
+                scores(step + 1, 0)
+                if s_next:
+                    copy_first(step + 1, scalar_copy)
             if ok(c_proj):
                 project(c_proj)
             if ok(step - 1):
@@ -323,7 +348,7 @@ def tile_attention2_pa_t_kernel(tc, q, k, v, w_proj, out):
                 part = slice((step - 1) * 2 * P, step * 2 * P)
                 quantise(nc, w_codes[:, part], w_scales[:, part], w_grouped[:, part].rearrange("p c t -> p (c t)"))
             if b < FRAMES:
-                group_v(b, j)
+                group_v(b, j, nc.vector if False else nc.gpsimd)
             for c, i in adds[added : added + (8 if tail else 3)]:
                 if exps.index((c, min(i, 1))) < done_early:
                     add(c, i)
@@ -331,28 +356,26 @@ def tile_attention2_pa_t_kernel(tc, q, k, v, w_proj, out):
             if ok(step):
                 maximum(step, 3)
                 subtract(step, 0)
-            if ok(c_norm):
+            if ok(c_norm) and not late:
                 normalise(c_norm, (0,))
             if not tail:
-                for c in logs[1:2]:
+                for c in logs[1:3]:
                     logarithm(c)
                 if ok(c_att):
                     regroup_o(c_att)
-                for c in logs[2:]:
+                for c in logs[3:]:
                     logarithm(c)
-            if step + 1 < CHUNKS:
-                scores(step + 1, 0)
-                if s_next:
-                    copy_first(step + 1, scalar_copy)
             if ok(c_proj) and not CHUNKS <= step < CHUNKS + 2:
-                store(c_proj, (scalar_copy, scalar_copy))
+                store(c_proj, (scalar_copy, vector_copy if shared else scalar_copy))
             for c, half in todo[len(early) :]:
                 exponential(c, half)
-            for h in range(1, HEADS):
+            for h in (1, 2, 3):
                 if ok(step):
                     subtract(step, h)
                 if step + 1 < CHUNKS:
                     scores(step + 1, h)
+            if ok(c_norm) and late:
+                normalise(c_norm, (0,))
             if step < W_GROUPS // 2:
                 turn_w(2 * step)
                 turn_w(2 * step + 1)

@@ -326,20 +326,13 @@ def tile_attention2_pa_t_kernel(tc, q, k, v, w_proj, out):
                 normalise(c_att, (2, 3))
             if ok(c_norm) and not tail:
                 turn_inverse(c_norm, "inv")
-            if 6 <= step < CHUNKS:
-                keep_warm(0)
             if ok(step):
                 maximum(step, 2)
             if CHUNKS < step <= CHUNKS + 2:
                 store(c_proj - 1, (vector_copy, vector_copy))
-            if ok(c_att):
+            if ok(c_att) and tail:
                 attend(c_att)
-                if tail:
-                    regroup_o(c_att)
-            if step + 1 < CHUNKS:
-                scores(step + 1, 0)
-                if s_next:
-                    copy_first(step + 1, scalar_copy)
+                regroup_o(c_att)
             if ok(c_proj):
                 project(c_proj)
             if ok(step - 1):
@@ -347,6 +340,8 @@ def tile_attention2_pa_t_kernel(tc, q, k, v, w_proj, out):
             if 0 < step <= W_GROUPS // 2:
                 part = slice((step - 1) * 2 * P, step * 2 * P)
                 quantise(nc, w_codes[:, part], w_scales[:, part], w_grouped[:, part].rearrange("p c t -> p (c t)"))
+            if ok(c_att) and not tail:
+                attend(c_att)
             if b < FRAMES:
                 group_v(b, j, nc.vector if False else nc.gpsimd)
             for c, i in adds[added : added + (8 if tail else 3)]:
@@ -365,6 +360,10 @@ def tile_attention2_pa_t_kernel(tc, q, k, v, w_proj, out):
                     regroup_o(c_att)
                 for c in logs[3:]:
                     logarithm(c)
+            if step + 1 < CHUNKS:
+                scores(step + 1, 0)
+                if s_next:
+                    copy_first(step + 1, scalar_copy)
             if ok(c_proj) and not CHUNKS <= step < CHUNKS + 2:
                 store(c_proj, (scalar_copy, vector_copy if shared else scalar_copy))
             for c, half in todo[len(early) :]:

@@ -71,7 +71,9 @@ def tile_attention2_pa_t_kernel(tc, q, k, v, w_proj, out):
 
         rows_of, turned_of, tr_ps_of, v_rows_of, v_grouped_of, v_mx_of = {}, {}, {}, {}, {}, {}
         s_of, first_of, top_of, shifted_of, e_of, sums_of, inverse_of = {}, {}, {}, {}, {}, {}, {}
-        inv_ps_of, attn_of, o_ps_of, o_mx_of, out_ps_of, out_rows_of = {}, {}, {}, {}, {}, {}
+        inv_ps_of, attn_of, o_ps_of, out_ps_of = {}, {}, {}, {}
+
+        vector_copy, scalar_copy = nc.vector.tensor_copy, nc.scalar.copy
 
         def ok(c):
             return 0 <= c < CHUNKS
@@ -108,9 +110,9 @@ def tile_attention2_pa_t_kernel(tc, q, k, v, w_proj, out):
                     nc.tensor.transpose(out=tr_ps[:, i, j, :], in_=rows[:, first + i, j, :], identity=ident[:])
             tr_ps_of[b, quarter] = (turned[:, first : first + 2, :, :], tr_ps)
 
-        def turned_copy(b, quarter, copy):
+        def turned_copy(b, quarter):
             turned, tr_ps = tr_ps_of[b, quarter]
-            copy(out=turned, in_=tr_ps[:])
+            scalar_copy(out=turned, in_=tr_ps[:])
 
         def turn_first_queries(first, tiles, bank, copy):
             q_rows, qT = rows_of[0][1], turned_of[0][1]
@@ -127,10 +129,10 @@ def tile_attention2_pa_t_kernel(tc, q, k, v, w_proj, out):
                 nc.tensor.transpose(out=w_ps[:, t, :], in_=w_rows[:, g, t * P : (t + 1) * P], identity=ident[:])
             nc.scalar.copy(out=w_grouped[:, g * P : (g + 1) * P, :], in_=w_ps[:].rearrange("p t c -> p c t"))
 
-        def group_v(b, h, engine):
+        def group_v(b, h):
             v_grouped = const.tile([P, HEAD_DIM, PACK], BF16, align_bytes=64)
             v_grouped_of[b, h] = v_grouped
-            engine.tensor_scalar(
+            nc.gpsimd.tensor_scalar(
                 out=v_grouped[:], in0=v_rows_of[b][:, h].rearrange("p t d -> p d t"),
                 scalar1=1.0, scalar2=0.0, op0=ALU.mult, op1=ALU.add,
             )
@@ -179,7 +181,7 @@ def tile_attention2_pa_t_kernel(tc, q, k, v, w_proj, out):
 
         def add(c, i):
             if i == 0:
-                pair_sums = const.tile([P, 2, P, PACK], F32)
+                pair_sums = two.tile([P, 2, P, PACK], F32)
                 sums_of[c] = pair_sums
             if i < 2:
                 nc.gpsimd.tensor_tensor(out=sums_of[c][:, i], in0=e_of[c][:, 2 * i], in1=e_of[c][:, 2 * i + 1], op=ALU.add)
@@ -249,10 +251,6 @@ def tile_attention2_pa_t_kernel(tc, q, k, v, w_proj, out):
                 mx_pass(nc, out_ps[:], o_codes[:], o_scales[:], w_codes[:, cols], w_scales[:, cols])
                 out_ps_of[c, half] = out_ps
 
-        def keep_warm(half):
-            idle_ps = psum.tile([P, BANK], F32, tag=f"out{half}")
-            mx_pass(nc, idle_ps[:], w_codes[:, :P], w_scales[:, :P], w_codes[:, BANK:], w_scales[:, BANK:])
-
         def store(c, copies):
             out_rows = three.tile([P, OUT_CH], F32)
             for half in range(OUT_CH // BANK):
@@ -260,7 +258,6 @@ def tile_attention2_pa_t_kernel(tc, q, k, v, w_proj, out):
             nc.sync.dma_start(out=out[c // TILES].rearrange("(p j) c -> p j c", j=TILES)[:, c % TILES, :], in_=out_rows[:])
 
         turns = [(b, quarter) for b in range(1, FRAMES) for quarter in range(4)]
-        vector_copy, scalar_copy = nc.vector.tensor_copy, nc.scalar.copy
 
         load_qk(0)
         load_v(0)
@@ -268,46 +265,46 @@ def tile_attention2_pa_t_kernel(tc, q, k, v, w_proj, out):
         load_qk(1)
         for quarter in (0, 2):
             turn(0, quarter, f"s{quarter}")
-            turned_copy(0, quarter, scalar_copy)
+            turned_copy(0, quarter)
             turn_first_queries(quarter, slice(0, 1), f"s{quarter + 1}", vector_copy)
         for h in range(HEADS):
             scores(0, h)
         for quarter in (0, 2):
             turn_first_queries(quarter, slice(1, TILES), f"out{quarter // 2}", scalar_copy)
 
+        group_v(0, 0)
+
         exps = [(c, half) for c in range(CHUNKS) for half in range(2)]
         adds = [(c, i) for c in range(CHUNKS) for i in range(3)]
         done = added = 0
+
         for step in range(CHUNKS + LAG_PROJECT + 1):
             b, j = step // TILES, step % TILES
-            tail = step >= CHUNKS
             c_log, c_norm, c_att, c_proj = step - LAG_LOG, step - LAG_NORMALISE, step - LAG_ATTEND, step - LAG_PROJECT
+            drain = step >= CHUNKS
             phase = c_log % BATCH
             logs = list(range(c_log, c_log + BATCH)) if ok(c_log) and phase == 0 else []
-            quota = 4 if tail else (0, 2, 3, 3)[phase] if step >= BATCH - 1 else 2
+            quota = 4 if drain else (0, 2, 3, 3)[phase] if step >= BATCH - 1 else 2
             todo = [x for x in exps[done : done + quota] if x[0] < step]
-            early = todo[: 3]
-            done_early = done + len(early)
-            done += len(todo)
-            s_next = (phase == 2) and step + 1 < CHUNKS
-            late = phase == 1
-            shared = (False) and not tail
+            late_exps = todo[3:]
+            done_before, done_early, done = done, done + len(todo) - len(late_exps), done + len(todo)
 
             if j == 0 and b + 2 < FRAMES:
                 load_qk(b + 2)
             if j == 0 and b + 1 < FRAMES:
                 load_v(b + 1)
+
             if ok(step) and step not in first_of:
                 copy_first(step, vector_copy)
             if step < len(turns):
-                turn(*turns[step], "s0")
+                turn(*turns[step], "inv" if step < LAG_LOG else "s0")
             if ok(c_norm) and step <= CHUNKS:
                 invert(c_norm)
             for c in logs[:1]:
                 logarithm(c)
             if step < len(turns):
-                turned_copy(*turns[step], scalar_copy)
-            if tail:
+                turned_copy(*turns[step])
+            if drain:
                 for c in logs[1:]:
                     logarithm(c)
                 if ok(c_log):
@@ -316,44 +313,51 @@ def tile_attention2_pa_t_kernel(tc, q, k, v, w_proj, out):
                     turn_inverse(c_norm, ("s3", "inv")[step % 2])
                 if ok(c_log):
                     invert(c_log)
-            for c, half in early:
+            for c, half in todo[:3]:
                 exponential(c, half)
+
             if ok(c_att):
                 normalise(c_att, (1,))
             if ok(step):
                 maximum(step, 1)
             if ok(c_att):
                 normalise(c_att, (2, 3))
-            if ok(c_norm) and not tail:
+            if ok(c_norm) and not drain and phase != 1:
                 turn_inverse(c_norm, "inv")
             if ok(step):
                 maximum(step, 2)
             if CHUNKS < step <= CHUNKS + 2:
                 store(c_proj - 1, (vector_copy, vector_copy))
-            if ok(c_att) and tail:
+
+            if ok(c_att) and drain:
                 attend(c_att)
                 regroup_o(c_att)
             if ok(c_proj):
                 project(c_proj)
-            if ok(step - 1):
-                quantise_v((step - 1) // TILES, (step - 1) % TILES)
+            if ok(step):
+                quantise_v(b, j)
             if 0 < step <= W_GROUPS // 2:
                 part = slice((step - 1) * 2 * P, step * 2 * P)
                 quantise(nc, w_codes[:, part], w_scales[:, part], w_grouped[:, part].rearrange("p c t -> p (c t)"))
-            if ok(c_att) and not tail:
+            if ok(c_att) and not drain:
                 attend(c_att)
-            if b < FRAMES:
-                group_v(b, j, nc.vector if False else nc.gpsimd)
-            for c, i in adds[added : added + (8 if tail else 3)]:
-                if exps.index((c, min(i, 1))) < done_early:
-                    add(c, i)
-                    added += 1
+            if ok(c_norm) and not drain and phase == 1:
+                turn_inverse(c_norm, "inv")
+
+            if step + 1 < CHUNKS:
+                group_v((step + 1) // TILES, (step + 1) % TILES)
+            for c, i in adds[added : added + (8 if drain else 3)]:
+                if exps.index((c, min(i, 1))) >= (done_before if i == 2 else done_early):
+                    break
+                add(c, i)
+                added += 1
             if ok(step):
                 maximum(step, 3)
-                subtract(step, 0)
-            if ok(c_norm) and not late:
+                subtract(step, 0, in_psum=step < LAG_LOG)
+            if ok(c_norm) and phase != 1:
                 normalise(c_norm, (0,))
-            if not tail:
+
+            if not drain:
                 for c in logs[1:3]:
                     logarithm(c)
                 if ok(c_att):
@@ -362,21 +366,22 @@ def tile_attention2_pa_t_kernel(tc, q, k, v, w_proj, out):
                     logarithm(c)
             if step + 1 < CHUNKS:
                 scores(step + 1, 0)
-                if s_next:
+                if phase >= 2:
                     copy_first(step + 1, scalar_copy)
             if ok(c_proj) and not CHUNKS <= step < CHUNKS + 2:
-                store(c_proj, (scalar_copy, vector_copy if shared else scalar_copy))
-            for c, half in todo[len(early) :]:
+                store(c_proj, (scalar_copy, scalar_copy))
+            for c, half in late_exps:
                 exponential(c, half)
-            for h in (1, 2, 3):
+
+            for h in range(1, HEADS):
                 if ok(step):
                     subtract(step, h)
                 if step + 1 < CHUNKS:
                     scores(step + 1, h)
-            if ok(c_norm) and late:
+            if ok(c_norm) and phase == 1:
                 normalise(c_norm, (0,))
             if step < W_GROUPS // 2:
                 turn_w(2 * step)
                 turn_w(2 * step + 1)
-            if ok(c_log) and not tail:
+            if ok(c_log) and not drain:
                 turn_log(c_log, "o")

from contextlib import ExitStack

import concourse.mybir as mybir
from concourse.masks import make_identity

BF16 = mybir.dt.bfloat16
F32 = mybir.dt.float32
U32 = mybir.dt.uint32
U8 = mybir.dt.uint8
FP8X4 = mybir.dt.float8_e4m3fn_x4
ACT = mybir.ActivationFunctionType
ALU = mybir.AluOpType

P = 128
PACK = 4
FRAMES, HEADS, TOKENS, HEAD_DIM, OUT_CH = 8, 4, 512, 128, 1024
CHANNELS = HEADS * HEAD_DIM
TILES = TOKENS // P
BANK = 512
SCALE = HEAD_DIM**-0.5
CHUNKS = FRAMES * TILES
W_GROUPS = OUT_CH // P

BATCH = TILES

LAG_LOG = BATCH + 2
LAG_NORMALISE = LAG_LOG + 1
LAG_ATTEND = LAG_NORMALISE + 1
LAG_PROJECT = LAG_ATTEND + 1

ORDER = (1, 2, 3, 0)

FLOPS = 2 * FRAMES * HEADS * TOKENS * TOKENS * HEAD_DIM * 2 + 2 * FRAMES * TOKENS * CHANNELS * OUT_CH


def quantise(nc, codes, scales, grouped):
    nc.vector.quantize_mx(out=codes.bitcast(FP8X4), scales=scales, in_=grouped)


def mx_pass(nc, acc, lhs_codes, lhs_scales, rhs_codes, rhs_scales):
    nc.tensor.matmul_mx(
        out=acc,
        lhsT=lhs_codes.bitcast(FP8X4),
        lhsT_scale=lhs_scales,
        rhs=rhs_codes.bitcast(FP8X4),
        rhs_scale=rhs_scales,
        start=True,
        stop=True,
    )


def tile_attention2_pa_t_kernel(tc, q, k, v, w_proj, out):
    nc = tc.nc
    with ExitStack() as stack:
        stack.enter_context(tc.manual_schedule())
        const = stack.enter_context(tc.tile_pool(name="const", bufs=1))
        two = stack.enter_context(tc.tile_pool(name="two", bufs=2))
        three = stack.enter_context(tc.tile_pool(name="three", bufs=3))
        four = stack.enter_context(tc.tile_pool(name="four", bufs=4))
        deep = stack.enter_context(tc.tile_pool(name="deep", bufs=LAG_NORMALISE + 1))
        psum = stack.enter_context(tc.psum_pool(name="psum", bufs=1))

        ident = const.tile([P, P], BF16)
        make_identity(nc, ident[:])
        ident_f32 = const.tile([P, P], F32)
        make_identity(nc, ident_f32[:])
        w_codes = const.tile([P, OUT_CH], U32, align_bytes=64)
        w_scales = const.tile([P, OUT_CH], U8, align_bytes=64)
        w_rows = deep.tile([P, W_GROUPS, CHANNELS], BF16, align_bytes=64, tag="e")
        w_grouped = deep.tile([P, OUT_CH, PACK], BF16, align_bytes=64, tag="e")

        rows_of, turned_of, tr_ps_of, v_rows_of, v_grouped_of, v_mx_of = {}, {}, {}, {}, {}, {}
        s_of, first_of, top_of, shifted_of, e_of, sums_of, inverse_of = {}, {}, {}, {}, {}, {}, {}
        inv_ps_of, attn_of, o_ps_of, out_ps_of = {}, {}, {}, {}

        vector_copy, scalar_copy = nc.vector.tensor_copy, nc.scalar.copy

        def ok(c):
            return 0 <= c < CHUNKS

        def load(rows, src, b, heads):
            nc.sync.dma_start(
                out=rows[:, heads].rearrange("p h j d -> p h (j d)"),
                in_=src[b, heads].rearrange("h (p j) d -> p h (j d)", j=TILES),
            )

        def load_qk(b):
            k_rows = two.tile([P, HEADS, TILES, HEAD_DIM], BF16)
            q_rows = two.tile([P, HEADS, TILES, HEAD_DIM], BF16)
            rows_of[b] = (k_rows, q_rows)
            for i in range(2):
                for rows, source in ((k_rows, k), (q_rows, q)):
                    load(rows, source, b, slice(2 * i, 2 * i + 2))

        def load_v(b):
            v_rows = two.tile([P, HEADS, PACK, HEAD_DIM], BF16)
            v_rows_of[b] = v_rows
            load(v_rows, v, b, slice(0, HEADS))

        def turn(b, quarter, bank):
            if quarter == 0:
                kT = two.tile([P, HEADS, TILES, P], BF16)
                qT = two.tile([P, HEADS, TILES, P], BF16)
                turned_of[b] = (kT, qT)
            rows, turned = rows_of[b][quarter % 2], turned_of[b][quarter % 2]
            first = 2 * (quarter // 2)
            tr_ps = psum.tile([P, 2, TILES, P], BF16, tag=bank)
            for i in range(2):
                for j in range(TILES):
                    nc.tensor.transpose(out=tr_ps[:, i, j, :], in_=rows[:, first + i, j, :], identity=ident[:])
            tr_ps_of[b, quarter] = (turned[:, first : first + 2, :, :], tr_ps)

        def turned_copy(b, quarter):
            turned, tr_ps = tr_ps_of[b, quarter]
            scalar_copy(out=turned, in_=tr_ps[:])

        def turn_first_queries(first, tiles, bank, copy):
            q_rows, qT = rows_of[0][1], turned_of[0][1]
            heads, count = slice(first, first + 2), tiles.stop - tiles.start
            tr_ps = psum.tile([P, 2, count, P], BF16, tag=bank)
            for i in range(2):
                for j in range(count):
                    nc.tensor.transpose(out=tr_ps[:, i, j, :], in_=q_rows[:, first + i, tiles.start + j, :], identity=ident[:])
            copy(out=qT[:, heads, tiles, :], in_=tr_ps[:])

        def turn_w(g):
            w_ps = psum.tile([P, PACK, P], BF16, tag=f"out{g % 2}")
            for t in range(PACK):
                nc.tensor.transpose(out=w_ps[:, t, :], in_=w_rows[:, g, t * P : (t + 1) * P], identity=ident[:])
            nc.scalar.copy(out=w_grouped[:, g * P : (g + 1) * P, :], in_=w_ps[:].rearrange("p t c -> p c t"))

        def group_v(b, h):
            v_grouped = const.tile([P, HEAD_DIM, PACK], BF16, align_bytes=64)
            v_grouped_of[b, h] = v_grouped
            nc.gpsimd.tensor_scalar(
                out=v_grouped[:], in0=v_rows_of[b][:, h].rearrange("p t d -> p d t"),
                scalar1=1.0, scalar2=0.0, op0=ALU.mult, op1=ALU.add,
            )

        def quantise_v(b, h):
            if h == 0:
                v_codes = three.tile([P, HEADS * HEAD_DIM], U32, align_bytes=64)
                v_scales = three.tile([P, HEADS * HEAD_DIM], U8, align_bytes=64)
                v_mx_of[b] = (v_codes, v_scales)
            v_codes, v_scales = v_mx_of[b]
            cols = slice(h * HEAD_DIM, (h + 1) * HEAD_DIM)
            quantise(nc, v_codes[:, cols], v_scales[:, cols], v_grouped_of[b, h][:].rearrange("p d t -> p (d t)"))

        def scores(c, h):
            kT, qT = turned_of[c // TILES]
            s_ps = psum.tile([P, PACK, P], F32, tag=f"s{h}")
            for t in range(PACK):
                nc.tensor.matmul(out=s_ps[:, t, :], lhsT=kT[:, h, t, :], rhs=qT[:, h, c % TILES, :], start=True, stop=True)
            s_of[c, h] = s_ps[:].rearrange("p t n -> p n t")

        def copy_first(c, copy):
            first = four.tile([P, P, PACK], F32)
            copy(out=first[:], in_=s_of[c, 0])
            first_of[c] = first

        def maximum(c, h):
            top = (two if h == HEADS - 1 else const).tile([P, P, PACK], F32, tag=f"top{h}")
            before = first_of[c] if h == 1 else top_of[c]
            nc.vector.tensor_tensor(out=top[:], in0=s_of[c, h], in1=before[:], op=ALU.max)
            top_of[c] = top

        def subtract(c, h, in_psum=False):
            if c not in shifted_of:
                shifted = three.tile([P, HEADS, P, PACK], F32)
                shifted_of[c] = shifted
            engine = nc.gpsimd if h == 0 and not in_psum else nc.vector
            scores_h = first_of[c][:] if h == 0 and not in_psum else s_of[c, h]
            engine.tensor_tensor(out=shifted_of[c][:, ORDER.index(h)], in0=scores_h, in1=top_of[c][:], op=ALU.subtract)

        def exponential(c, half):
            if half == 0:
                e = deep.tile([P, HEADS, P, PACK], F32, align_bytes=64, tag="e")
                e_of[c] = e
            pair = slice(2 * half, 2 * half + 2)
            nc.scalar.activation(out=e_of[c][:, pair], in_=shifted_of[c][:, pair], func=ACT.Exp, scale=SCALE)

        def add(c, i):
            if i == 0:
                pair_sums = two.tile([P, 2, P, PACK], F32)
                sums_of[c] = pair_sums
            if i < 2:
                nc.gpsimd.tensor_tensor(out=sums_of[c][:, i], in0=e_of[c][:, 2 * i], in1=e_of[c][:, 2 * i + 1], op=ALU.add)
            else:
                total = deep.tile([P, P * PACK], F32)
                pair_sums = sums_of[c]
                nc.gpsimd.tensor_tensor(
                    out=total[:], in0=pair_sums[:, 0].rearrange("p n t -> p (n t)"), in1=pair_sums[:, 1].rearrange("p n t -> p (n t)"),
                    op=ALU.add,
                )
                sums_of[c] = total

        def logarithm(c):
            nc.scalar.activation(out=sums_of[c][:], in_=sums_of[c][:], func=ACT.Ln)

        def turn_log(c, bank):
            log_ps = psum.tile([P, PACK, P], F32, tag=bank)
            for i in range(PACK):
                nc.tensor.transpose(out=log_ps[:, i, :], in_=sums_of[c][:, i * P : (i + 1) * P], identity=ident_f32[:])
            inverse = two.tile([P, PACK, P], F32)
            inverse_of[c] = (log_ps, inverse)

        def invert(c):
            log_ps, inverse = inverse_of[c]
            nc.scalar.activation(out=inverse[:], in_=log_ps[:], func=ACT.Exp, scale=-1.0)

        def turn_inverse(c, bank):
            inv_ps = psum.tile([P, PACK, P], F32, tag=bank)
            for i in range(PACK):
                nc.tensor.transpose(out=inv_ps[:, i, :], in_=inverse_of[c][1][:, i, :], identity=ident_f32[:])
            inv_ps_of[c] = inv_ps

        def normalise(c, slots):
            if slots[0] == 0:
                attn = three.tile([P, HEADS, P * PACK], BF16, align_bytes=64)
                attn_of[c] = attn
            count = len(slots)
            part = slice(slots[0], slots[0] + count)
            nc.vector.tensor_tensor(
                out=attn_of[c][:, part], in0=e_of[c][:, part].rearrange("p h n t -> p h (n t)"),
                in1=inv_ps_of[c][:].rearrange("p i n -> p (i n)").unsqueeze(1).to_broadcast([P, count, P * PACK]), op=ALU.mult,
            )

        def attend(c):
            attn_codes = two.tile([P, HEADS * P], U32, align_bytes=64)
            attn_scales = two.tile([P, HEADS * P], U8, align_bytes=64)
            quantise(nc, attn_codes[:], attn_scales[:], attn_of[c][:].rearrange("p h m -> p (h m)"))
            v_codes, v_scales = v_mx_of[c // TILES]
            o_ps = psum.tile([P, HEADS, P], F32, tag="o")
            for slot, h in enumerate(ORDER):
                rhs, lhs = slice(slot * P, (slot + 1) * P), slice(h * P, (h + 1) * P)
                mx_pass(nc, o_ps[:, h, :], v_codes[:, lhs], v_scales[:, lhs], attn_codes[:, rhs], attn_scales[:, rhs])
            o_ps_of[c] = o_ps

        def regroup_o(c):
            o_grouped = three.tile([P, P, PACK], BF16, align_bytes=64)
            nc.scalar.copy(out=o_grouped[:], in_=o_ps_of[c][:].rearrange("p h n -> p n h"))
            o_ps_of[c] = o_grouped

        def project(c):
            o_codes = two.tile([P, P], U32, align_bytes=64)
            o_scales = two.tile([P, P], U8, align_bytes=64)
            quantise(nc, o_codes[:], o_scales[:], o_ps_of[c][:].rearrange("p n h -> p (n h)"))
            for half in range(OUT_CH // BANK):
                cols = slice(half * BANK, (half + 1) * BANK)
                out_ps = psum.tile([P, BANK], F32, tag=f"out{half}")
                mx_pass(nc, out_ps[:], o_codes[:], o_scales[:], w_codes[:, cols], w_scales[:, cols])
                out_ps_of[c, half] = out_ps

        def store(c, copies):
            out_rows = three.tile([P, OUT_CH], F32)
            for half in range(OUT_CH // BANK):
                copies[half](out=out_rows[:, half * BANK : (half + 1) * BANK], in_=out_ps_of[c, half][:])
            nc.sync.dma_start(out=out[c // TILES].rearrange("(p j) c -> p j c", j=TILES)[:, c % TILES, :], in_=out_rows[:])

        turns = [(b, quarter) for b in range(1, FRAMES) for quarter in range(4)]

        load_qk(0)
        load_v(0)
        nc.sync.dma_start(out=w_rows[:], in_=w_proj.rearrange("(g p) c -> p g c", p=P))
        load_qk(1)
        for quarter in (0, 2):
            turn(0, quarter, f"s{quarter}")
            turned_copy(0, quarter)
            turn_first_queries(quarter, slice(0, 1), f"s{quarter + 1}", vector_copy)
        for h in range(HEADS):
            scores(0, h)
        for quarter in (0, 2):
            turn_first_queries(quarter, slice(1, TILES), f"out{quarter // 2}", scalar_copy)

        group_v(0, 0)

        exps = [(c, half) for c in range(CHUNKS) for half in range(2)]
        adds = [(c, i) for c in range(CHUNKS) for i in range(3)]
        done = added = 0

        for step in range(CHUNKS + LAG_PROJECT + 1):
            b, j = step // TILES, step % TILES
            c_log, c_norm, c_att, c_proj = step - LAG_LOG, step - LAG_NORMALISE, step - LAG_ATTEND, step - LAG_PROJECT
            drain = step >= CHUNKS
            phase = c_log % BATCH
            logs = list(range(c_log, c_log + BATCH)) if ok(c_log) and phase == 0 else []
            quota = 4 if drain else (0, 2, 3, 3)[phase] if step >= BATCH - 1 else 2
            todo = [x for x in exps[done : done + quota] if x[0] < step]
            late_exps = todo[3:]
            done_before, done_early, done = done, done + len(todo) - len(late_exps), done + len(todo)

            if j == 0 and b + 2 < FRAMES:
                load_qk(b + 2)
            if j == 0 and b + 1 < FRAMES:
                load_v(b + 1)

            if ok(step) and step not in first_of:
                copy_first(step, vector_copy)
            if step < len(turns):
                turn(*turns[step], "inv" if step < LAG_LOG else "s0")
            if ok(c_norm) and step <= CHUNKS:
                invert(c_norm)
            for c in logs[:1]:
                logarithm(c)
            if step < len(turns):
                turned_copy(*turns[step])
            if drain:
                for c in logs[1:]:
                    logarithm(c)
                if ok(c_log):
                    turn_log(c_log, ("s1", "s2")[step % 2])
                if ok(c_norm):
                    turn_inverse(c_norm, ("s3", "inv")[step % 2])
                if ok(c_log):
                    invert(c_log)
            for c, half in todo[:3]:
                exponential(c, half)

            if ok(c_att):
                normalise(c_att, (1,))
            if ok(step):
                maximum(step, 1)
            if ok(c_att):
                normalise(c_att, (2, 3))
            if ok(c_norm) and not drain and phase != 1:
                turn_inverse(c_norm, "inv")
            if ok(step):
                maximum(step, 2)
            if CHUNKS < step <= CHUNKS + 2:
                store(c_proj - 1, (vector_copy, vector_copy))

            if ok(c_att) and drain:
                attend(c_att)
                regroup_o(c_att)
            if ok(c_proj):
                project(c_proj)
            if ok(step):
                quantise_v(b, j)
            if 0 < step <= W_GROUPS // 2:
                part = slice((step - 1) * 2 * P, step * 2 * P)
                quantise(nc, w_codes[:, part], w_scales[:, part], w_grouped[:, part].rearrange("p c t -> p (c t)"))
            if ok(c_att) and not drain:
                attend(c_att)
            if ok(c_norm) and not drain and phase == 1:
                turn_inverse(c_norm, "inv")

            if step + 1 < CHUNKS:
                group_v((step + 1) // TILES, (step + 1) % TILES)
            for c, i in adds[added : added + (8 if drain else 3)]:
                if exps.index((c, min(i, 1))) >= (done_before if i == 2 else done_early):
                    break
                add(c, i)
                added += 1
            if ok(step):
                maximum(step, 3)
                subtract(step, 0, in_psum=step < LAG_LOG)
            if ok(c_norm) and phase != 1:
                normalise(c_norm, (0,))

            if not drain:
                for c in logs[1:3]:
                    logarithm(c)
                if ok(c_att):
                    regroup_o(c_att)
                for c in logs[3:]:
                    logarithm(c)
            if step + 1 < CHUNKS:
                scores(step + 1, 0)
                if phase >= 2:
                    copy_first(step + 1, scalar_copy)
            if ok(c_proj) and not CHUNKS <= step < CHUNKS + 2:
                store(c_proj, (scalar_copy, scalar_copy))
            for c, half in late_exps:
                exponential(c, half)

            for h in range(1, HEADS):
                if ok(step):
                    subtract(step, h)
                if step + 1 < CHUNKS:
                    scores(step + 1, h)
            if ok(c_norm) and phase == 1:
                normalise(c_norm, (0,))
            if step < W_GROUPS // 2:
                turn_w(2 * step)
                turn_w(2 * step + 1)
            if ok(c_log) and not drain:
                turn_log(c_log, "o")
